import numpy as np
import ml_dtypes


def mxq(x, axis, fmt="e4m3"):
    dtype, down = {"e4m3": (ml_dtypes.float8_e4m3fn, 7), "e5m2": (ml_dtypes.float8_e5m2, 14)}[fmt]
    v = np.moveaxis(np.asarray(x, np.float32).astype(ml_dtypes.bfloat16).astype(np.float64), axis, -1)
    blocks = v.reshape(v.shape[:-1] + (-1, 32))
    amax = np.abs(blocks).max(-1, keepdims=True)
    byte = np.maximum(np.where(amax > 0, np.frexp(amax)[1] - 1 + 127, 0) - down, 1)
    scale = np.exp2(byte - 127.0)
    codes = (blocks / scale).astype(np.float32).astype(dtype).astype(np.float64)
    return np.moveaxis((codes * scale).reshape(v.shape), -1, axis)


WIDE = False


def mx_kscale(k):
    if not WIDE:
        return np.ones(k)
    levels = np.array([10, -10, 5, -5, 0])
    a = np.random.permutation(np.resize(levels, k // 512 * 4)).reshape(k // 512, 4)
    idx = np.arange(k)
    return np.exp2(a[idx // 512, idx % 128 // 32])


BF16 = ml_dtypes.bfloat16


def bf(x):
    return np.asarray(x, np.float32).astype(BF16)


def f64(x):
    return np.asarray(x).astype(np.float64)


E2M1 = np.array([0.0, 0.5, 1.0, 1.5, 2.0, 3.0, 4.0, 6.0, -0.0, -0.5, -1.0, -1.5, -2.0, -3.0, -4.0, -6.0])


def pack_weight(w, fmt):
    k, n = w.shape
    w = f64(bf(w)).reshape(k // 32, 32, n)
    amax = np.abs(w).max(1)
    if fmt == "e4m3":
        byte = np.frexp(amax)[1] - 1 + 127 - 7
    else:
        mant, ex = np.frexp(amax / 6.0)
        byte = np.where(mant > 0.5, ex, ex - 1) + 127
    byte = np.clip(np.where(amax > 0, byte, 1), 1, 254)
    scaled = (w * np.exp2(127.0 - byte)[:, None, :]).reshape(k, n).astype(np.float32)
    by_word = np.ascontiguousarray(scaled.reshape(k // 512, 128, 4, n).transpose(0, 1, 3, 2))
    if fmt == "e4m3":
        words = by_word.astype(ml_dtypes.float8_e4m3fn).view(np.uint8)
    else:
        c = by_word.astype(ml_dtypes.float4_e2m1fn).view(np.uint8) & 0xF
        words = c[..., 0::2] | (c[..., 1::2] << 4)
    return np.ascontiguousarray(words), np.ascontiguousarray(byte.astype(np.uint8).reshape(k // 512, 16, n))


def unpack_weight(words, scales, fmt):
    g, p, n, _ = words.shape
    if fmt == "e4m3":
        vals = np.ascontiguousarray(words).view(ml_dtypes.float8_e4m3fn).astype(np.float64)
    else:
        nib = np.empty((g, p, n, 4), np.uint8)
        nib[..., 0::2] = words & 0xF
        nib[..., 1::2] = words >> 4
        vals = E2M1[nib]
    vals = vals * np.repeat(np.exp2(scales.astype(np.float64) - 127.0), 8, axis=1)[..., None]
    return vals.transpose(0, 1, 3, 2).reshape(g * 512, n)


B, S, P, D, H, HD = 1, 512, 1024, 2048, 16, 128
T = P + S


def heads(t):
    return t.reshape(B, -1, H, HD).transpose(0, 2, 1, 3)


def setup_inputs():
    s = mx_kscale(D)
    x = bf(np.random.standard_normal((B, S, D)) * s)
    q = bf(np.random.standard_normal((B, H, S, HD)) * 1.5)
    k_new = bf(np.random.standard_normal((B, H, S, HD)) * 1.5)
    past_k = bf(np.random.standard_normal((B, H, P, HD)) * 1.5)
    past_v = bf(np.random.standard_normal((B, H, P, HD)))
    Wv = np.random.standard_normal((D, D)) / np.sqrt(D) / s[None, :]
    Wv_words, Wv_scales = pack_weight(Wv.T, "e4m3")
    bv = bf(np.random.standard_normal(D) * 0.3)
    return {
        "x": x,
        "q": q,
        "k_new": k_new,
        "past_k": past_k,
        "past_v": past_v,
        "Wv_words": Wv_words,
        "Wv_scales": Wv_scales,
        "bv": bv,
    }


def reference(x, q, k_new, past_k, past_v, Wv_words, Wv_scales, bv):
    v_new = heads((mxq(f64(x), 2, "e4m3") @ unpack_weight(Wv_words, Wv_scales, "e4m3")) + f64(bv))
    v_cached = np.concatenate([f64(past_v), v_new], axis=2)
    qf = f64(q)
    scores = np.concatenate([qf @ f64(past_k).transpose(0, 1, 3, 2), qf @ f64(k_new).transpose(0, 1, 3, 2)], axis=3) * (1.0 / np.sqrt(HD))
    q_pos = np.arange(T - S, T)[:, None]
    k_pos = np.arange(T)[None, :]
    scores = np.where(q_pos >= k_pos, scores, -np.inf)
    e = np.exp(scores - scores.max(-1, keepdims=True))
    out = (mxq(e, 3, "e4m3") @ mxq(v_cached, 2, "e4m3")) / e.sum(-1, keepdims=True)
    return out.transpose(0, 2, 1, 3).reshape(B, S, D)

@@ -1,0 +1,309 @@
+from contextlib import ExitStack
+import math
+
+import concourse.mybir as mybir
+from concourse.masks import make_identity
+
+F32 = mybir.dt.float32
+BF16 = mybir.dt.bfloat16
+I32 = mybir.dt.int32
+U32 = mybir.dt.uint32
+U8 = mybir.dt.uint8
+FP8X4 = mybir.dt.float8_e4m3fn_x4
+ALU = mybir.AluOpType
+ACT = mybir.ActivationFunctionType
+AX = mybir.AxisListType
+
+P = 128
+HEADS = 16
+NEW = 512
+PAST = 1024
+FEATURES = 2048
+BANK = 512
+K_PASS = 512
+Q_BLOCKS = NEW // P
+KEY_PASSES = (PAST + NEW) // K_PASS
+X_PASSES = FEATURES // K_PASS
+HEADS_PER_W_LOAD = 4
+SCALE = 1.0 / math.sqrt(P)
+MASKED = -1.0e10
+
+FLOPS = 2 * NEW * FEATURES * FEATURES + 2 * 2 * HEADS * NEW * (PAST + NEW) * P
+
+
+def tile_flashattentionmodule_pa_kernel(
+    tc, x, q, k_new, past_k, past_v, Wv_words, Wv_scales, bv, out
+):
+    nc = tc.nc
+    with ExitStack() as ctx:
+        const = ctx.enter_context(tc.tile_pool(name="const", bufs=1))
+        raw = ctx.enter_context(tc.tile_pool(name="raw", bufs=3))
+        work = ctx.enter_context(tc.tile_pool(name="work", bufs=2))
+        small = ctx.enter_context(tc.tile_pool(name="small", bufs=4))
+        score_banks = ctx.enter_context(tc.psum_pool(name="score_banks", bufs=5))
+        other_banks = ctx.enter_context(tc.psum_pool(name="other_banks", bufs=3))
+
+        ident_bf = const.tile([P, P], BF16, name="ident_bf")
+        make_identity(nc, ident_bf[:])
+        ident_f32 = const.tile([P, P], F32, name="ident_f32")
+        make_identity(nc, ident_f32[:])
+        causal_f32 = const.tile([P, P], F32, name="causal_f32")
+        nc.gpsimd.memset(causal_f32[:], 0.0)
+        nc.gpsimd.affine_select(
+            out=causal_f32[:],
+            in_=causal_f32[:],
+            compare_op=ALU.is_ge,
+            fill=MASKED,
+            base=0,
+            pattern=[[-1, P]],
+            channel_multiplier=1,
+        )
+        causal = const.tile([P, P], BF16, name="causal")
+        nc.vector.tensor_copy(out=causal[:], in_=causal_f32[:])
+
+        w_scales = const.tile([P, FEATURES], U8, name="w_scales", align_bytes=64)
+        nc.vector.memset(w_scales[:].bitcast(I32), 0)
+
+        e_tiles = []
+        for i in range(Q_BLOCKS):
+            e_tile = const.tile([P, PAST + NEW], BF16, name="e_block%d" % i)
+            if i + 1 < Q_BLOCKS:
+                nc.vector.memset(e_tile[:, PAST + P * (i + 1) :], 0.0)
+            e_tiles.append(e_tile)
+
+        x_rows = const.tile([P, 4, FEATURES], BF16, name="x_rows")
+        x_words = const.tile([P, X_PASSES, NEW], U32, name="x_words", align_bytes=64)
+        x_scales = const.tile([P, X_PASSES, NEW], U8, name="x_scales", align_bytes=64)
+        w_words = const.tile([P, X_PASSES, FEATURES], U32, name="w_words", align_bytes=64)
+        bias = const.tile([P, FEATURES], BF16, name="bias")
+
+        def load_head(h):
+            k_past = raw.tile([P, 2, 4, P], BF16, tag="k_past", name="k_past")
+            nc.sync.dma_start(
+                out=k_past[:], in_=past_k[0, h].rearrange("(a r c) d -> r a c d", a=2, c=4)
+            )
+            k_fresh = raw.tile([P, Q_BLOCKS, P], BF16, tag="k_fresh", name="k_fresh")
+            nc.sync.dma_start(out=k_fresh[:], in_=k_new[0, h].rearrange("(j r) d -> r j d", r=P))
+            q_rows = raw.tile([P, Q_BLOCKS, P], BF16, tag="q_rows", name="q_rows")
+            nc.sync.dma_start(out=q_rows[:], in_=q[0, h].rearrange("(i r) d -> r i d", r=P))
+            v_past = raw.tile([P, 8, P], BF16, tag="v_past", name="v_past")
+            nc.sync.dma_start(out=v_past[:], in_=past_v[0, h].rearrange("(p j) d -> p j d", j=8))
+            return k_past, k_fresh, q_rows, v_past
+
+        def load_x():
+            by_part = x[0].rearrange("(u m c) k -> u c m k", u=2, c=2)
+            for u in range(2):
+                for c in range(2):
+                    nc.sync.dma_start(out=x_rows[:, 2 * u + c, :], in_=by_part[u, c])
+
+        def load_w_scales():
+            for quadrant in range(4):
+                nc.sync.dma_start(
+                    out=w_scales[32 * quadrant : 32 * quadrant + 16, :].bitcast(I32),
+                    in_=Wv_scales[:, 4 * quadrant : 4 * quadrant + 4, :].bitcast(I32),
+                )
+
+        def load_w(part):
+            cols = slice(part * HEADS_PER_W_LOAD * P, (part + 1) * HEADS_PER_W_LOAD * P)
+            nc.sync.dma_start(
+                out=w_words[:, :, cols].bitcast(I32),
+                in_=Wv_words.rearrange("g p n t -> p g (n t)").bitcast(I32)[:, :, cols],
+            )
+
+        def quantise_x():
+            for g in range(X_PASSES):
+                grouped = work.tile([P, NEW, 4], BF16, tag="x_grouped", name="x_grouped", align_bytes=64)
+                for half in range(2):
+                    turned = other_banks.tile([P, 2, 2, P], F32, tag="bank", name="x_turned")
+                    for part in range(2):
+                        words = x_rows[:, 2 * half + part, :].bitcast(F32)
+                        for u in range(2):
+                            nc.tensor.transpose(
+                                turned[:, part, u, :],
+                                words[:, 256 * g + u : 256 * (g + 1) : 2],
+                                ident_f32[:],
+                            )
+                    nc.scalar.copy(
+                        out=grouped[:, 256 * half : 256 * (half + 1), :]
+                        .bitcast(F32)
+                        .rearrange("p (part m) u -> p part m u", part=2),
+                        in_=turned[:].rearrange("p part u m -> p part m u"),
+                    )
+                nc.vector.quantize_mx(
+                    out=x_words[:, g, :].bitcast(FP8X4),
+                    scales=x_scales[:, g, :],
+                    in_=grouped[:].rearrange("p m t -> p (m t)"),
+                )
+
+        def turn_keys_and_queries(k_past, k_fresh, q_rows):
+            turned_all = work.tile([P, 2 * PAST], BF16, tag="kq_turned", name="kq_turned")
+            bank = other_banks.tile([P, 8, P], BF16, tag="bank", name="k_bank")
+            for c in range(4):
+                for a in range(2):
+                    nc.tensor.transpose(bank[:, 2 * c + a, :], k_past[:, a, c, :], ident_bf[:])
+            nc.scalar.copy(out=turned_all[:, 0:PAST], in_=bank[:].rearrange("p j r -> p (j r)"))
+            bank = other_banks.tile([P, 8, P], BF16, tag="bank", name="kq_bank")
+            for j in range(Q_BLOCKS):
+                nc.tensor.transpose(bank[:, j, :], k_fresh[:, j, :], ident_bf[:])
+            for i in range(Q_BLOCKS):
+                nc.tensor.transpose(bank[:, Q_BLOCKS + i, :], q_rows[:, i, :], ident_bf[:])
+            nc.scalar.copy(out=turned_all[:, PAST:], in_=bank[:].rearrange("p j r -> p (j r)"))
+            return turned_all
+
+        def quantise_values(h, v_past):
+            grouped = work.tile([P, KEY_PASSES, P, 4], BF16, tag="v_grouped", name="v_grouped", align_bytes=64)
+            v_words = work.tile([P, KEY_PASSES, P], U32, tag="v_words", name="v_words", align_bytes=64)
+            v_scales = work.tile([P, KEY_PASSES, P], U8, tag="v_scales", name="v_scales", align_bytes=64)
+            by_pass = v_past[:].rearrange("p (c g u) d -> p g d u c", c=2, g=2)
+            for g in range(2):
+                nc.vector.tensor_copy(
+                    out=grouped[:, g].rearrange("p d (u c) -> p d u c", u=2), in_=by_pass[:, g]
+                )
+            nc.vector.quantize_mx(
+                out=v_words[:, 0:2, :].rearrange("p g d -> p (g d)").bitcast(FP8X4),
+                scales=v_scales[:, 0:2, :].rearrange("p g d -> p (g d)"),
+                in_=grouped[:, 0:2].rearrange("p g d t -> p (g d t)"),
+            )
+            y = other_banks.tile([P, 4, P], F32, tag="bank", name="y")
+            cols = slice(P * h, P * (h + 1))
+            for t in range(4):
+                for g in range(X_PASSES):
+                    nc.tensor.matmul_mx(
+                        out=y[:, t, :],
+                        lhsT=x_words[:, g, P * t : P * (t + 1)].bitcast(FP8X4),
+                        lhsT_scale=x_scales[:, g, P * t : P * (t + 1)],
+                        rhs=w_words[:, g, cols].bitcast(FP8X4),
+                        rhs_scale=w_scales[4 * g : P, cols],
+                        start=(g == 0),
+                        stop=(g == X_PASSES - 1),
+                    )
+            nc.vector.tensor_tensor(
+                out=grouped[:, 2],
+                in0=y[:].rearrange("p t d -> p d t"),
+                in1=bias[:, cols].unsqueeze(2).to_broadcast([P, P, 4]),
+                op=ALU.add,
+            )
+            nc.vector.quantize_mx(
+                out=v_words[:, 2, :].bitcast(FP8X4),
+                scales=v_scales[:, 2, :],
+                in_=grouped[:, 2].rearrange("p d t -> p (d t)"),
+            )
+            return v_words, v_scales
+
+        def scores(turned_all, i):
+            queries = turned_all[:, PAST + NEW + P * i : PAST + NEW + P * (i + 1)]
+            banks = []
+            for c in range(PAST // BANK):
+                s = score_banks.tile([P, BANK], F32, tag="s", name="s_past")
+                nc.tensor.matmul(
+                    out=s[:], lhsT=queries, rhs=turned_all[:, BANK * c : BANK * (c + 1)], start=True, stop=True
+                )
+                banks.append((s, BANK))
+            visible = P * (i + 1)
+            s = score_banks.tile([P, BANK], F32, tag="s", name="s_new")
+            nc.tensor.matmul(
+                out=s[:, 0:visible], lhsT=queries, rhs=turned_all[:, PAST : PAST + visible], start=True, stop=False
+            )
+            nc.tensor.matmul(
+                out=s[:, visible - P : visible], lhsT=ident_bf[:], rhs=causal[:], start=False, stop=True
+            )
+            banks.append((s, visible))
+            return banks
+
+        def softmax(banks, i, sums):
+            bank_max = small.tile([P, len(banks)], F32, tag="bank_max", name="bank_max")
+            for c, (s, width) in enumerate(banks):
+                nc.vector.reduce_max(out=bank_max[:, c : c + 1], in_=s[:, 0:width], axis=AX.X)
+            row_max = small.tile([P, 1], F32, tag="row_max", name="row_max")
+            nc.vector.reduce_max(out=row_max[:], in_=bank_max[:], axis=AX.X)
+            shift = small.tile([P, 1], F32, tag="shift", name="shift")
+            nc.vector.tensor_scalar_mul(out=shift[:], in0=row_max[:], scalar1=-SCALE)
+            for c, (s, width) in enumerate(banks):
+                nc.scalar.activation(
+                    out=e_tiles[i][:, BANK * c : BANK * c + width],
+                    in_=s[:, 0:width],
+                    func=ACT.Exp,
+                    bias=shift[:],
+                    scale=SCALE,
+                    accum_out=sums[:, i, c : c + 1],
+                )
+
+        def quantise_e(i, e_words, e_scales):
+            pairs = e_tiles[i][:].bitcast(F32)
+            grouped = work.tile([P, KEY_PASSES, P, 4], BF16, tag="e_grouped", name="e_grouped", bufs=3, align_bytes=64)
+            for first, count in ((0, 2), (2, 1)):
+                turned = other_banks.tile([P, count, 2, P], F32, tag="bank", name="e_turned")
+                for g in range(count):
+                    for u in range(2):
+                        start = P * (2 * (first + g) + u)
+                        nc.tensor.transpose(turned[:, g, u, :], pairs[:, start : start + P], ident_f32[:])
+                nc.scalar.copy(
+                    out=grouped[:, first : first + count].bitcast(F32),
+                    in_=turned[:].rearrange("p g u q -> p g q u"),
+                )
+                nc.vector.quantize_mx(
+                    out=e_words[:, i, first : first + count, :].rearrange("p g q -> p (g q)").bitcast(FP8X4),
+                    scales=e_scales[:, i, first : first + count, :].rearrange("p g q -> p (g q)"),
+                    in_=grouped[:, first : first + count].rearrange("p g q t -> p (g q t)"),
+                )
+
+        def weighted_values(h, e_words, e_scales, v_words, v_scales, sums):
+            o = other_banks.tile([P, Q_BLOCKS, P], F32, tag="bank", name="o")
+            for i in range(Q_BLOCKS):
+                for g in range(KEY_PASSES):
+                    nc.tensor.matmul_mx(
+                        out=o[:, i, :],
+                        lhsT=e_words[:, i, g, :].bitcast(FP8X4),
+                        lhsT_scale=e_scales[:, i, g, :],
+                        rhs=v_words[:, g, :].bitcast(FP8X4),
+                        rhs_scale=v_scales[:, g, :],
+                        start=(g == 0),
+                        stop=(g == KEY_PASSES - 1),
+                    )
+            row_sum = small.tile([P, Q_BLOCKS], F32, tag="row_sum", name="row_sum")
+            nc.vector.reduce_sum(out=row_sum[:], in_=sums[:], axis=AX.X)
+            inverse = small.tile([P, Q_BLOCKS], F32, tag="inverse", name="inverse")
+            nc.vector.reciprocal(out=inverse[:], in_=row_sum[:])
+            result = work.tile([P, Q_BLOCKS, P], F32, tag="result", name="result")
+            nc.vector.tensor_tensor(
+                out=result[:],
+                in0=o[:],
+                in1=inverse[:].unsqueeze(2).to_broadcast([P, Q_BLOCKS, P]),
+                op=ALU.mult,
+            )
+            nc.sync.dma_start(
+                out=out[0].rearrange("(i r) (h d) -> h r i d", r=P, d=P)[h], in_=result[:]
+            )
+
+        loaded = {0: load_head(0)}
+        load_x()
+        load_w_scales()
+        load_w(0)
+        nc.sync.dma_start(out=bias[:], in_=bv.partition_broadcast(P))
+        loaded[1] = load_head(1)
+
+        turned = {0: turn_keys_and_queries(*loaded[0][0:3])}
+        banks = scores(turned[0], 0)
+        for h in range(HEADS):
+            e_words = work.tile([P, Q_BLOCKS, KEY_PASSES, P], U32, tag="e_words", name="e_words", align_bytes=64)
+            e_scales = work.tile([P, Q_BLOCKS, KEY_PASSES, P], U8, tag="e_scales", name="e_scales", align_bytes=64)
+            sums = small.tile([P, Q_BLOCKS, KEY_PASSES], F32, tag="sums", name="sums")
+            for i in range(Q_BLOCKS):
+                current = banks
+                if i + 1 < Q_BLOCKS:
+                    banks = scores(turned[h], i + 1)
+                elif h + 1 < HEADS:
+                    banks = scores(turned[h + 1], 0)
+                softmax(current, i, sums)
+                quantise_e(i, e_words, e_scales)
+                if i == 0 and h + 2 < HEADS:
+                    if (h + 2) % HEADS_PER_W_LOAD == 0:
+                        load_w((h + 2) // HEADS_PER_W_LOAD)
+                    loaded[h + 2] = load_head(h + 2)
+                if i == 1 and h + 1 < HEADS:
+                    turned[h + 1] = turn_keys_and_queries(*loaded[h + 1][0:3])
+                if i == 2:
+                    if h == 0:
+                        quantise_x()
+                    v_words, v_scales = quantise_values(h, loaded[h][3])
+            weighted_values(h, e_words, e_scales, v_words, v_scales, sums)

@@ -25,6 +25,9 @@ Q_BLOCKS = NEW // P
 KEY_PASSES = (PAST + NEW) // K_PASS
 X_PASSES = FEATURES // K_PASS
 HEADS_PER_W_LOAD = 4
+UNITS = HEADS * Q_BLOCKS
+UNIT_BANKS = 3
+SCORE_BANKS = 5
 SCALE = 1.0 / math.sqrt(P)
 MASKED = -1.0e10
 
@@ -36,12 +39,13 @@ def tile_flashattentionmodule_pa_kernel(
 ):
     nc = tc.nc
     with ExitStack() as ctx:
+        ctx.enter_context(tc.manual_schedule())
         const = ctx.enter_context(tc.tile_pool(name="const", bufs=1))
         raw = ctx.enter_context(tc.tile_pool(name="raw", bufs=3))
         work = ctx.enter_context(tc.tile_pool(name="work", bufs=2))
         small = ctx.enter_context(tc.tile_pool(name="small", bufs=4))
-        score_banks = ctx.enter_context(tc.psum_pool(name="score_banks", bufs=5))
-        other_banks = ctx.enter_context(tc.psum_pool(name="other_banks", bufs=3))
+        score_pool = ctx.enter_context(tc.psum_pool(name="score_pool", bufs=SCORE_BANKS))
+        other_pool = ctx.enter_context(tc.psum_pool(name="other_pool", bufs=8 - SCORE_BANKS))
 
         ident_bf = const.tile([P, P], BF16, name="ident_bf")
         make_identity(nc, ident_bf[:])
@@ -77,18 +81,27 @@ def tile_flashattentionmodule_pa_kernel(
         w_words = const.tile([P, X_PASSES, FEATURES], U32, name="w_words", align_bytes=64)
         bias = const.tile([P, FEATURES], BF16, name="bias")
 
+        k_past, k_fresh, q_rows, v_past = {}, {}, {}, {}
+        columns = {}
+        v_grouped, v_words, v_scales = {}, {}, {}
+        e_words, e_scales, sums = {}, {}, {}
+        y, o = {}, {}
+        score_banks = {}
+        shift = {}
+        e_turned = {}
+        e_grouped = {}
+
         def load_head(h):
-            k_past = raw.tile([P, 2, 4, P], BF16, tag="k_past", name="k_past")
+            k_past[h] = raw.tile([P, 2, 4, P], BF16, tag="k_past", name="k_past")
             nc.sync.dma_start(
-                out=k_past[:], in_=past_k[0, h].rearrange("(a r c) d -> r a c d", a=2, c=4)
+                out=k_past[h][:], in_=past_k[0, h].rearrange("(a r c) d -> r a c d", a=2, c=4)
             )
-            k_fresh = raw.tile([P, Q_BLOCKS, P], BF16, tag="k_fresh", name="k_fresh")
-            nc.sync.dma_start(out=k_fresh[:], in_=k_new[0, h].rearrange("(j r) d -> r j d", r=P))
-            q_rows = raw.tile([P, Q_BLOCKS, P], BF16, tag="q_rows", name="q_rows")
-            nc.sync.dma_start(out=q_rows[:], in_=q[0, h].rearrange("(i r) d -> r i d", r=P))
-            v_past = raw.tile([P, 8, P], BF16, tag="v_past", name="v_past")
-            nc.sync.dma_start(out=v_past[:], in_=past_v[0, h].rearrange("(p j) d -> p j d", j=8))
-            return k_past, k_fresh, q_rows, v_past
+            q_rows[h] = raw.tile([P, Q_BLOCKS, P], BF16, tag="q_rows", name="q_rows")
+            nc.sync.dma_start(out=q_rows[h][:], in_=q[0, h].rearrange("(i r) d -> r i d", r=P))
+            k_fresh[h] = raw.tile([P, Q_BLOCKS, P], BF16, tag="k_fresh", name="k_fresh")
+            nc.sync.dma_start(out=k_fresh[h][:], in_=k_new[0, h].rearrange("(j r) d -> r j d", r=P))
+            v_past[h] = raw.tile([P, 8, P], BF16, tag="v_past", name="v_past")
+            nc.sync.dma_start(out=v_past[h][:], in_=past_v[0, h].rearrange("(p j) d -> p j d", j=8))
 
         def load_x():
             by_part = x[0].rearrange("(u m c) k -> u c m k", u=2, c=2)
@@ -112,64 +125,67 @@ def tile_flashattentionmodule_pa_kernel(
 
         def quantise_x():
             for g in range(X_PASSES):
-                grouped = work.tile([P, NEW, 4], BF16, tag="x_grouped", name="x_grouped", align_bytes=64)
+                x_grouped = work.tile([P, NEW, 4], BF16, tag="x_grouped", name="x_grouped", align_bytes=64)
                 for half in range(2):
-                    turned = other_banks.tile([P, 2, 2, P], F32, tag="bank", name="x_turned")
+                    x_turned = other_pool.tile([P, 2, 2, P], F32, tag="bank", name="x_turned")
                     for part in range(2):
-                        words = x_rows[:, 2 * half + part, :].bitcast(F32)
+                        pairs = x_rows[:, 2 * half + part, :].bitcast(F32)
                         for u in range(2):
                             nc.tensor.transpose(
-                                turned[:, part, u, :],
-                                words[:, 256 * g + u : 256 * (g + 1) : 2],
+                                x_turned[:, part, u, :],
+                                pairs[:, 256 * g + u : 256 * (g + 1) : 2],
                                 ident_f32[:],
                             )
                     nc.scalar.copy(
-                        out=grouped[:, 256 * half : 256 * (half + 1), :]
+                        out=x_grouped[:, 256 * half : 256 * (half + 1), :]
                         .bitcast(F32)
                         .rearrange("p (part m) u -> p part m u", part=2),
-                        in_=turned[:].rearrange("p part u m -> p part m u"),
+                        in_=x_turned[:].rearrange("p part u m -> p part m u"),
                     )
                 nc.vector.quantize_mx(
                     out=x_words[:, g, :].bitcast(FP8X4),
                     scales=x_scales[:, g, :],
-                    in_=grouped[:].rearrange("p m t -> p (m t)"),
+                    in_=x_grouped[:].rearrange("p m t -> p (m t)"),
                 )
 
-        def turn_keys_and_queries(k_past, k_fresh, q_rows):
-            turned_all = work.tile([P, 2 * PAST], BF16, tag="kq_turned", name="kq_turned")
-            bank = other_banks.tile([P, 8, P], BF16, tag="bank", name="k_bank")
+        def turn_cached_keys(h):
+            columns[h] = work.tile([P, 2 * PAST], BF16, tag="columns", name="columns")
+            bank = other_pool.tile([P, 8, P], BF16, tag="bank", name="k_bank")
             for c in range(4):
                 for a in range(2):
-                    nc.tensor.transpose(bank[:, 2 * c + a, :], k_past[:, a, c, :], ident_bf[:])
-            nc.scalar.copy(out=turned_all[:, 0:PAST], in_=bank[:].rearrange("p j r -> p (j r)"))
-            bank = other_banks.tile([P, 8, P], BF16, tag="bank", name="kq_bank")
-            for j in range(Q_BLOCKS):
-                nc.tensor.transpose(bank[:, j, :], k_fresh[:, j, :], ident_bf[:])
-            for i in range(Q_BLOCKS):
-                nc.tensor.transpose(bank[:, Q_BLOCKS + i, :], q_rows[:, i, :], ident_bf[:])
-            nc.scalar.copy(out=turned_all[:, PAST:], in_=bank[:].rearrange("p j r -> p (j r)"))
-            return turned_all
+                    nc.tensor.transpose(bank[:, 2 * c + a, :], k_past[h][:, a, c, :], ident_bf[:])
+            nc.scalar.copy(out=columns[h][:, 0:PAST], in_=bank[:].rearrange("p j r -> p (j r)"))
 
-        def quantise_values(h, v_past):
-            grouped = work.tile([P, KEY_PASSES, P, 4], BF16, tag="v_grouped", name="v_grouped", align_bytes=64)
-            v_words = work.tile([P, KEY_PASSES, P], U32, tag="v_words", name="v_words", align_bytes=64)
-            v_scales = work.tile([P, KEY_PASSES, P], U8, tag="v_scales", name="v_scales", align_bytes=64)
-            by_pass = v_past[:].rearrange("p (c g u) d -> p g d u c", c=2, g=2)
+        def turn_new_keys_and_queries(h):
+            bank = other_pool.tile([P, 8, P], BF16, tag="bank", name="kq_bank")
+            for j in range(Q_BLOCKS):
+                nc.tensor.transpose(bank[:, j, :], k_fresh[h][:, j, :], ident_bf[:])
+            for i in range(Q_BLOCKS):
+                nc.tensor.transpose(bank[:, Q_BLOCKS + i, :], q_rows[h][:, i, :], ident_bf[:])
+            nc.scalar.copy(out=columns[h][:, PAST:], in_=bank[:].rearrange("p j r -> p (j r)"))
+
+        def quantise_cached_values(h):
+            v_grouped[h] = work.tile([P, KEY_PASSES, P, 4], BF16, tag="v_grouped", name="v_grouped", align_bytes=64)
+            v_words[h] = work.tile([P, KEY_PASSES, P], U32, tag="v_words", name="v_words", align_bytes=64)
+            v_scales[h] = work.tile([P, KEY_PASSES, P], U8, tag="v_scales", name="v_scales", align_bytes=64)
+            by_pass = v_past[h][:].rearrange("p (c g u) d -> p g d u c", c=2, g=2)
             for g in range(2):
                 nc.vector.tensor_copy(
-                    out=grouped[:, g].rearrange("p d (u c) -> p d u c", u=2), in_=by_pass[:, g]
+                    out=v_grouped[h][:, g].rearrange("p d (u c) -> p d u c", u=2), in_=by_pass[:, g]
                 )
             nc.vector.quantize_mx(
-                out=v_words[:, 0:2, :].rearrange("p g d -> p (g d)").bitcast(FP8X4),
-                scales=v_scales[:, 0:2, :].rearrange("p g d -> p (g d)"),
-                in_=grouped[:, 0:2].rearrange("p g d t -> p (g d t)"),
+                out=v_words[h][:, 0:2, :].rearrange("p g d -> p (g d)").bitcast(FP8X4),
+                scales=v_scales[h][:, 0:2, :].rearrange("p g d -> p (g d)"),
+                in_=v_grouped[h][:, 0:2].rearrange("p g d t -> p (g d t)"),
             )
-            y = other_banks.tile([P, 4, P], F32, tag="bank", name="y")
+
+        def project_new_values(h):
+            y[h] = other_pool.tile([P, 4, P], F32, tag="bank", name="y")
             cols = slice(P * h, P * (h + 1))
             for t in range(4):
                 for g in range(X_PASSES):
                     nc.tensor.matmul_mx(
-                        out=y[:, t, :],
+                        out=y[h][:, t, :],
                         lhsT=x_words[:, g, P * t : P * (t + 1)].bitcast(FP8X4),
                         lhsT_scale=x_scales[:, g, P * t : P * (t + 1)],
                         rhs=w_words[:, g, cols].bitcast(FP8X4),
@@ -177,97 +193,124 @@ def tile_flashattentionmodule_pa_kernel(
                         start=(g == 0),
                         stop=(g == X_PASSES - 1),
                     )
+
+        def quantise_new_values(h):
             nc.vector.tensor_tensor(
-                out=grouped[:, 2],
-                in0=y[:].rearrange("p t d -> p d t"),
-                in1=bias[:, cols].unsqueeze(2).to_broadcast([P, P, 4]),
+                out=v_grouped[h][:, 2],
+                in0=y[h][:].rearrange("p t d -> p d t"),
+                in1=bias[:, P * h : P * (h + 1)].unsqueeze(2).to_broadcast([P, P, 4]),
                 op=ALU.add,
             )
             nc.vector.quantize_mx(
-                out=v_words[:, 2, :].bitcast(FP8X4),
-                scales=v_scales[:, 2, :],
-                in_=grouped[:, 2].rearrange("p d t -> p (d t)"),
+                out=v_words[h][:, 2, :].bitcast(FP8X4),
+                scales=v_scales[h][:, 2, :],
+                in_=v_grouped[h][:, 2].rearrange("p d t -> p (d t)"),
             )
-            return v_words, v_scales
 
-        def scores(turned_all, i):
-            queries = turned_all[:, PAST + NEW + P * i : PAST + NEW + P * (i + 1)]
-            banks = []
-            for c in range(PAST // BANK):
-                s = score_banks.tile([P, BANK], F32, tag="s", name="s_past")
+        def score_bank(unit, c):
+            h, i = divmod(unit, Q_BLOCKS)
+            queries = columns[h][:, PAST + NEW + P * i : PAST + NEW + P * (i + 1)]
+            s = score_pool.tile([P, BANK], F32, tag="s", name="s")
+            if c < PAST // BANK:
+                width = BANK
                 nc.tensor.matmul(
-                    out=s[:], lhsT=queries, rhs=turned_all[:, BANK * c : BANK * (c + 1)], start=True, stop=True
+                    out=s[:], lhsT=queries, rhs=columns[h][:, BANK * c : BANK * (c + 1)], start=True, stop=True
                 )
-                banks.append((s, BANK))
-            visible = P * (i + 1)
-            s = score_banks.tile([P, BANK], F32, tag="s", name="s_new")
-            nc.tensor.matmul(
-                out=s[:, 0:visible], lhsT=queries, rhs=turned_all[:, PAST : PAST + visible], start=True, stop=False
-            )
-            nc.tensor.matmul(
-                out=s[:, visible - P : visible], lhsT=ident_bf[:], rhs=causal[:], start=False, stop=True
-            )
-            banks.append((s, visible))
-            return banks
+            else:
+                width = P * (i + 1)
+                nc.tensor.matmul(
+                    out=s[:, 0:width], lhsT=queries, rhs=columns[h][:, PAST : PAST + width], start=True, stop=False
+                )
+                nc.tensor.matmul(
+                    out=s[:, width - P : width], lhsT=ident_bf[:], rhs=causal[:], start=False, stop=True
+                )
+            score_banks[(unit, c)] = (s, width)
 
-        def softmax(banks, i, sums):
-            bank_max = small.tile([P, len(banks)], F32, tag="bank_max", name="bank_max")
-            for c, (s, width) in enumerate(banks):
+        def row_maximum(unit):
+            bank_max = small.tile([P, UNIT_BANKS], F32, tag="bank_max", name="bank_max")
+            for c in range(UNIT_BANKS):
+                s, width = score_banks[(unit, c)]
                 nc.vector.reduce_max(out=bank_max[:, c : c + 1], in_=s[:, 0:width], axis=AX.X)
             row_max = small.tile([P, 1], F32, tag="row_max", name="row_max")
             nc.vector.reduce_max(out=row_max[:], in_=bank_max[:], axis=AX.X)
-            shift = small.tile([P, 1], F32, tag="shift", name="shift")
-            nc.vector.tensor_scalar_mul(out=shift[:], in0=row_max[:], scalar1=-SCALE)
-            for c, (s, width) in enumerate(banks):
+            shift[unit] = small.tile([P, 1], F32, tag="shift", name="shift")
+            nc.vector.tensor_scalar_mul(out=shift[unit][:], in0=row_max[:], scalar1=-SCALE)
+
+        def exponentials(unit):
+            h, i = divmod(unit, Q_BLOCKS)
+            if i == 0:
+                sums[h] = small.tile([P, Q_BLOCKS, UNIT_BANKS], F32, tag="sums", name="sums")
+            for c in range(UNIT_BANKS):
+                s, width = score_banks[(unit, c)]
                 nc.scalar.activation(
                     out=e_tiles[i][:, BANK * c : BANK * c + width],
                     in_=s[:, 0:width],
                     func=ACT.Exp,
-                    bias=shift[:],
+                    bias=shift[unit][:],
                     scale=SCALE,
-                    accum_out=sums[:, i, c : c + 1],
+                    accum_out=sums[h][:, i, c : c + 1],
                 )
 
-        def quantise_e(i, e_words, e_scales):
-            pairs = e_tiles[i][:].bitcast(F32)
-            grouped = work.tile([P, KEY_PASSES, P, 4], BF16, tag="e_grouped", name="e_grouped", bufs=3, align_bytes=64)
+        def turn_e(unit):
+            pairs = e_tiles[unit % Q_BLOCKS][:].bitcast(F32)
+            e_turned[unit] = []
             for first, count in ((0, 2), (2, 1)):
-                turned = other_banks.tile([P, count, 2, P], F32, tag="bank", name="e_turned")
+                bank = other_pool.tile([P, count, 2, P], F32, tag="bank", name="e_bank")
                 for g in range(count):
                     for u in range(2):
-                        start = P * (2 * (first + g) + u)
-                        nc.tensor.transpose(turned[:, g, u, :], pairs[:, start : start + P], ident_f32[:])
+                        left = P * (2 * (first + g) + u)
+                        nc.tensor.transpose(bank[:, g, u, :], pairs[:, left : left + P], ident_f32[:])
+                e_turned[unit].append((first, count, bank))
+
+        def group_e(unit):
+            e_grouped[unit] = work.tile(
+                [P, KEY_PASSES, P, 4], BF16, tag="e_grouped", name="e_grouped", bufs=3, align_bytes=64
+            )
+            for first, count, bank in e_turned[unit]:
                 nc.scalar.copy(
-                    out=grouped[:, first : first + count].bitcast(F32),
-                    in_=turned[:].rearrange("p g u q -> p g q u"),
-                )
-                nc.vector.quantize_mx(
-                    out=e_words[:, i, first : first + count, :].rearrange("p g q -> p (g q)").bitcast(FP8X4),
-                    scales=e_scales[:, i, first : first + count, :].rearrange("p g q -> p (g q)"),
-                    in_=grouped[:, first : first + count].rearrange("p g q t -> p (g q t)"),
+                    out=e_grouped[unit][:, first : first + count].bitcast(F32),
+                    in_=bank[:].rearrange("p g u q -> p g q u"),
                 )
 
-        def weighted_values(h, e_words, e_scales, v_words, v_scales, sums):
-            o = other_banks.tile([P, Q_BLOCKS, P], F32, tag="bank", name="o")
+        def quantise_e(unit):
+            h, i = divmod(unit, Q_BLOCKS)
+            if i == 0:
+                e_words[h] = work.tile(
+                    [P, Q_BLOCKS, KEY_PASSES, P], U32, tag="e_words", name="e_words", align_bytes=64
+                )
+                e_scales[h] = work.tile(
+                    [P, Q_BLOCKS, KEY_PASSES, P], U8, tag="e_scales", name="e_scales", align_bytes=64
+                )
+            for first, count in ((0, 2), (2, 1)):
+                nc.vector.quantize_mx(
+                    out=e_words[h][:, i, first : first + count, :].rearrange("p g q -> p (g q)").bitcast(FP8X4),
+                    scales=e_scales[h][:, i, first : first + count, :].rearrange("p g q -> p (g q)"),
+                    in_=e_grouped[unit][:, first : first + count].rearrange("p g q t -> p (g q t)"),
+                )
+
+        def weighted_values(h):
+            o[h] = other_pool.tile([P, Q_BLOCKS, P], F32, tag="bank", name="o")
             for i in range(Q_BLOCKS):
                 for g in range(KEY_PASSES):
                     nc.tensor.matmul_mx(
-                        out=o[:, i, :],
-                        lhsT=e_words[:, i, g, :].bitcast(FP8X4),
-                        lhsT_scale=e_scales[:, i, g, :],
-                        rhs=v_words[:, g, :].bitcast(FP8X4),
-                        rhs_scale=v_scales[:, g, :],
+                        out=o[h][:, i, :],
+                        lhsT=e_words[h][:, i, g, :].bitcast(FP8X4),
+                        lhsT_scale=e_scales[h][:, i, g, :],
+                        rhs=v_words[h][:, g, :].bitcast(FP8X4),
+                        rhs_scale=v_scales[h][:, g, :],
                         start=(g == 0),
                         stop=(g == KEY_PASSES - 1),
                     )
+
+        def normalise_and_store(h):
             row_sum = small.tile([P, Q_BLOCKS], F32, tag="row_sum", name="row_sum")
-            nc.vector.reduce_sum(out=row_sum[:], in_=sums[:], axis=AX.X)
+            nc.vector.reduce_sum(out=row_sum[:], in_=sums[h][:], axis=AX.X)
             inverse = small.tile([P, Q_BLOCKS], F32, tag="inverse", name="inverse")
             nc.vector.reciprocal(out=inverse[:], in_=row_sum[:])
             result = work.tile([P, Q_BLOCKS, P], F32, tag="result", name="result")
             nc.vector.tensor_tensor(
                 out=result[:],
-                in0=o[:],
+                in0=o[h][:],
                 in1=inverse[:].unsqueeze(2).to_broadcast([P, Q_BLOCKS, P]),
                 op=ALU.mult,
             )
@@ -275,35 +318,59 @@ def tile_flashattentionmodule_pa_kernel(
                 out=out[0].rearrange("(i r) (h d) -> h r i d", r=P, d=P)[h], in_=result[:]
             )
 
-        loaded = {0: load_head(0)}
+        def is_unit(unit):
+            return 0 <= unit < UNITS
+
+        def is_head(h):
+            return 0 <= h < HEADS
+
+        load_head(0)
         load_x()
         load_w_scales()
         load_w(0)
         nc.sync.dma_start(out=bias[:], in_=bv.partition_broadcast(P))
-        loaded[1] = load_head(1)
+        load_head(1)
+        turn_cached_keys(0)
+        turn_new_keys_and_queries(0)
 
-        turned = {0: turn_keys_and_queries(*loaded[0][0:3])}
-        banks = scores(turned[0], 0)
-        for h in range(HEADS):
-            e_words = work.tile([P, Q_BLOCKS, KEY_PASSES, P], U32, tag="e_words", name="e_words", align_bytes=64)
-            e_scales = work.tile([P, Q_BLOCKS, KEY_PASSES, P], U8, tag="e_scales", name="e_scales", align_bytes=64)
-            sums = small.tile([P, Q_BLOCKS, KEY_PASSES], F32, tag="sums", name="sums")
-            for i in range(Q_BLOCKS):
-                current = banks
-                if i + 1 < Q_BLOCKS:
-                    banks = scores(turned[h], i + 1)
-                elif h + 1 < HEADS:
-                    banks = scores(turned[h + 1], 0)
-                softmax(current, i, sums)
-                quantise_e(i, e_words, e_scales)
-                if i == 0 and h + 2 < HEADS:
+        for now in range(-2, UNITS + Q_BLOCKS):
+            h, block = divmod(now, Q_BLOCKS)
+            refills = [divmod(UNIT_BANKS * now + SCORE_BANKS + n, UNIT_BANKS) for n in range(UNIT_BANKS)]
+            if is_unit(now - 1):
+                turn_e(now - 1)
+            if is_unit(now - 2):
+                quantise_e(now - 2)
+            if is_unit(now):
+                exponentials(now)
+            if is_unit(now - 1):
+                group_e(now - 1)
+            if is_unit(refills[0][0]):
+                score_bank(*refills[0])
+
+            if block == 0 and is_head(h) and is_head(h + 1):
+                turn_cached_keys(h + 1)
+            if block == 1 and is_head(h) and is_head(h + 1):
+                turn_new_keys_and_queries(h + 1)
+            if block == 2 and is_head(h - 1):
+                project_new_values(h - 1)
+            if block == 3 and h == 0:
+                quantise_x()
+            if block == 3 and is_head(h - 1):
+                weighted_values(h - 1)
+
+            for unit, c in refills[1:]:
+                if is_unit(unit):
+                    score_bank(unit, c)
+            if is_unit(now + 1):
+                row_maximum(now + 1)
+
+            if block == 0 and is_head(h):
+                quantise_cached_values(h)
+                if is_head(h + 2):
                     if (h + 2) % HEADS_PER_W_LOAD == 0:
                         load_w((h + 2) // HEADS_PER_W_LOAD)
-                    loaded[h + 2] = load_head(h + 2)
-                if i == 1 and h + 1 < HEADS:
-                    turned[h + 1] = turn_keys_and_queries(*loaded[h + 1][0:3])
-                if i == 2:
-                    if h == 0:
-                        quantise_x()
-                    v_words, v_scales = quantise_values(h, loaded[h][3])
-            weighted_values(h, e_words, e_scales, v_words, v_scales, sums)
+                    load_head(h + 2)
+            if block == 2 and is_head(h - 1):
+                quantise_new_values(h - 1)
+            if block == 3 and is_head(h - 1):
+                normalise_and_store(h - 1)

@@ -28,6 +28,7 @@ HEADS_PER_W_LOAD = 4
 UNITS = HEADS * Q_BLOCKS
 UNIT_BANKS = 3
 SCORE_BANKS = 5
+QUARTER_ORDER = (3, 0, 1, 2)
 SCALE = 1.0 / math.sqrt(P)
 MASKED = -1.0e10
 
@@ -84,11 +85,11 @@ def tile_flashattentionmodule_pa_kernel(
         k_past, k_fresh, q_rows, v_past = {}, {}, {}, {}
         columns = {}
         v_grouped, v_words, v_scales = {}, {}, {}
-        e_words, e_scales, sums = {}, {}, {}
+        e_words, e_scales, sums, inverse, result = {}, {}, {}, {}, {}
+        x_grouped = {}
         y, o = {}, {}
         score_banks = {}
         shift = {}
-        e_turned = {}
         e_grouped = {}
 
         def load_head(h):
@@ -123,84 +124,92 @@ def tile_flashattentionmodule_pa_kernel(
                 in_=Wv_words.rearrange("g p n t -> p g (n t)").bitcast(I32)[:, :, cols],
             )
 
-        def quantise_x():
-            for g in range(X_PASSES):
-                x_grouped = work.tile([P, NEW, 4], BF16, tag="x_grouped", name="x_grouped", align_bytes=64)
-                for half in range(2):
-                    x_turned = other_pool.tile([P, 2, 2, P], F32, tag="bank", name="x_turned")
-                    for part in range(2):
-                        pairs = x_rows[:, 2 * half + part, :].bitcast(F32)
-                        for u in range(2):
-                            nc.tensor.transpose(
-                                x_turned[:, part, u, :],
-                                pairs[:, 256 * g + u : 256 * (g + 1) : 2],
-                                ident_f32[:],
-                            )
-                    nc.scalar.copy(
-                        out=x_grouped[:, 256 * half : 256 * (half + 1), :]
-                        .bitcast(F32)
-                        .rearrange("p (part m) u -> p part m u", part=2),
-                        in_=x_turned[:].rearrange("p part u m -> p part m u"),
-                    )
-                nc.vector.quantize_mx(
-                    out=x_words[:, g, :].bitcast(FP8X4),
-                    scales=x_scales[:, g, :],
-                    in_=x_grouped[:].rearrange("p m t -> p (m t)"),
+        def turn_x(g):
+            x_grouped[g] = work.tile([P, NEW, 4], BF16, tag="x_grouped", name="x_grouped", align_bytes=64)
+            for half in range(2):
+                bank = other_pool.tile([P, 2, 2, P], F32, tag="bank", name="x_bank")
+                for part in range(2):
+                    pairs = x_rows[:, 2 * half + part, :].bitcast(F32)
+                    for u in range(2):
+                        nc.tensor.transpose(
+                            bank[:, part, u, :], pairs[:, 256 * g + u : 256 * (g + 1) : 2], ident_f32[:]
+                        )
+                nc.scalar.copy(
+                    out=x_grouped[g][:, 256 * half : 256 * (half + 1), :]
+                    .bitcast(F32)
+                    .rearrange("p (part m) u -> p part m u", part=2),
+                    in_=bank[:].rearrange("p part u m -> p part m u"),
                 )
 
-        def turn_cached_keys(h):
-            columns[h] = work.tile([P, 2 * PAST], BF16, tag="columns", name="columns")
-            bank = other_pool.tile([P, 8, P], BF16, tag="bank", name="k_bank")
-            for c in range(4):
-                for a in range(2):
-                    nc.tensor.transpose(bank[:, 2 * c + a, :], k_past[h][:, a, c, :], ident_bf[:])
-            nc.scalar.copy(out=columns[h][:, 0:PAST], in_=bank[:].rearrange("p j r -> p (j r)"))
+        def quantise_x(g):
+            nc.vector.quantize_mx(
+                out=x_words[:, g, :].bitcast(FP8X4),
+                scales=x_scales[:, g, :],
+                in_=x_grouped[g][:].rearrange("p m t -> p (m t)"),
+            )
 
-        def turn_new_keys_and_queries(h):
-            bank = other_pool.tile([P, 8, P], BF16, tag="bank", name="kq_bank")
-            for j in range(Q_BLOCKS):
-                nc.tensor.transpose(bank[:, j, :], k_fresh[h][:, j, :], ident_bf[:])
-            for i in range(Q_BLOCKS):
-                nc.tensor.transpose(bank[:, Q_BLOCKS + i, :], q_rows[h][:, i, :], ident_bf[:])
-            nc.scalar.copy(out=columns[h][:, PAST:], in_=bank[:].rearrange("p j r -> p (j r)"))
+        def operand_rows(h, position):
+            if position < 8:
+                c, a = divmod(position, 2)
+                return k_past[h][:, a, c, :]
+            if position < 12:
+                return k_fresh[h][:, position - 8, :]
+            return q_rows[h][:, position - 12, :]
+
+        def turn_operands(h, quarter, half_bank):
+            for j in range(4):
+                nc.tensor.transpose(half_bank[:, j, :], operand_rows(h, 4 * quarter + j), ident_bf[:])
+
+        def copy_operands(h, quarter, half_bank):
+            nc.scalar.copy(
+                out=columns[h][:, BANK * quarter : BANK * (quarter + 1)],
+                in_=half_bank.rearrange("p j r -> p (j r)"),
+            )
+
+        def group_cached_values(h, g):
+            if g == 0:
+                v_grouped[h] = work.tile(
+                    [P, KEY_PASSES, P, 4], BF16, tag="v_grouped", name="v_grouped", align_bytes=64
+                )
+            nc.vector.tensor_copy(
+                out=v_grouped[h][:, g].rearrange("p d (u c) -> p d u c", u=2),
+                in_=v_past[h][:].rearrange("p (c g u) d -> p g d u c", c=2, g=2)[:, g],
+            )
 
         def quantise_cached_values(h):
-            v_grouped[h] = work.tile([P, KEY_PASSES, P, 4], BF16, tag="v_grouped", name="v_grouped", align_bytes=64)
             v_words[h] = work.tile([P, KEY_PASSES, P], U32, tag="v_words", name="v_words", align_bytes=64)
             v_scales[h] = work.tile([P, KEY_PASSES, P], U8, tag="v_scales", name="v_scales", align_bytes=64)
-            by_pass = v_past[h][:].rearrange("p (c g u) d -> p g d u c", c=2, g=2)
-            for g in range(2):
-                nc.vector.tensor_copy(
-                    out=v_grouped[h][:, g].rearrange("p d (u c) -> p d u c", u=2), in_=by_pass[:, g]
-                )
             nc.vector.quantize_mx(
                 out=v_words[h][:, 0:2, :].rearrange("p g d -> p (g d)").bitcast(FP8X4),
                 scales=v_scales[h][:, 0:2, :].rearrange("p g d -> p (g d)"),
                 in_=v_grouped[h][:, 0:2].rearrange("p g d t -> p (g d t)"),
             )
 
-        def project_new_values(h):
-            y[h] = other_pool.tile([P, 4, P], F32, tag="bank", name="y")
+        def project_new_values(h, u):
+            y[(h, u)] = other_pool.tile([P, 2, P], F32, tag="bank", name="y")
             cols = slice(P * h, P * (h + 1))
-            for t in range(4):
+            for c in range(2):
+                tokens = slice(P * (2 * u + c), P * (2 * u + c + 1))
                 for g in range(X_PASSES):
                     nc.tensor.matmul_mx(
-                        out=y[h][:, t, :],
-                        lhsT=x_words[:, g, P * t : P * (t + 1)].bitcast(FP8X4),
-                        lhsT_scale=x_scales[:, g, P * t : P * (t + 1)],
+                        out=y[(h, u)][:, c, :],
+                        lhsT=x_words[:, g, tokens].bitcast(FP8X4),
+                        lhsT_scale=x_scales[:, g, tokens],
                         rhs=w_words[:, g, cols].bitcast(FP8X4),
                         rhs_scale=w_scales[4 * g : P, cols],
                         start=(g == 0),
                         stop=(g == X_PASSES - 1),
                     )
 
-        def quantise_new_values(h):
+        def group_new_values(h, u):
             nc.vector.tensor_tensor(
-                out=v_grouped[h][:, 2],
-                in0=y[h][:].rearrange("p t d -> p d t"),
-                in1=bias[:, P * h : P * (h + 1)].unsqueeze(2).to_broadcast([P, P, 4]),
+                out=v_grouped[h][:, 2, :, 2 * u : 2 * u + 2],
+                in0=y[(h, u)][:].rearrange("p c d -> p d c"),
+                in1=bias[:, P * h : P * (h + 1)].unsqueeze(2).to_broadcast([P, P, 2]),
                 op=ALU.add,
             )
+
+        def quantise_new_values(h):
             nc.vector.quantize_mx(
                 out=v_words[h][:, 2, :].bitcast(FP8X4),
                 scales=v_scales[h][:, 2, :],
@@ -228,13 +237,19 @@ def tile_flashattentionmodule_pa_kernel(
 
         def row_maximum(unit):
             bank_max = small.tile([P, UNIT_BANKS], F32, tag="bank_max", name="bank_max")
-            for c in range(UNIT_BANKS):
+            for c in range(2):
                 s, width = score_banks[(unit, c)]
                 nc.vector.reduce_max(out=bank_max[:, c : c + 1], in_=s[:, 0:width], axis=AX.X)
-            row_max = small.tile([P, 1], F32, tag="row_max", name="row_max")
-            nc.vector.reduce_max(out=row_max[:], in_=bank_max[:], axis=AX.X)
+            cached = small.tile([P, 1], F32, tag="cached", name="cached")
+            nc.vector.tensor_scalar(
+                out=cached[:], in0=bank_max[:, 0:1], scalar1=bank_max[:, 1:2], scalar2=-SCALE, op0=ALU.max, op1=ALU.mult
+            )
+            s, width = score_banks[(unit, 2)]
+            nc.vector.reduce_max(out=bank_max[:, 2:3], in_=s[:, 0:width], axis=AX.X)
             shift[unit] = small.tile([P, 1], F32, tag="shift", name="shift")
-            nc.vector.tensor_scalar_mul(out=shift[unit][:], in0=row_max[:], scalar1=-SCALE)
+            nc.vector.tensor_scalar(
+                out=shift[unit][:], in0=bank_max[:, 2:3], scalar1=-SCALE, scalar2=cached[:], op0=ALU.mult, op1=ALU.min
+            )
 
         def exponentials(unit):
             h, i = divmod(unit, Q_BLOCKS)
@@ -251,35 +266,27 @@ def tile_flashattentionmodule_pa_kernel(
                     accum_out=sums[h][:, i, c : c + 1],
                 )
 
-        def turn_e(unit):
+        def turn_e(unit, first, count, bank):
             pairs = e_tiles[unit % Q_BLOCKS][:].bitcast(F32)
-            e_turned[unit] = []
-            for first, count in ((0, 2), (2, 1)):
-                bank = other_pool.tile([P, count, 2, P], F32, tag="bank", name="e_bank")
-                for g in range(count):
-                    for u in range(2):
-                        left = P * (2 * (first + g) + u)
-                        nc.tensor.transpose(bank[:, g, u, :], pairs[:, left : left + P], ident_f32[:])
-                e_turned[unit].append((first, count, bank))
+            for g in range(count):
+                for u in range(2):
+                    left = P * (2 * (first + g) + u)
+                    nc.tensor.transpose(bank[:, g, u, :], pairs[:, left : left + P], ident_f32[:])
 
-        def group_e(unit):
-            e_grouped[unit] = work.tile(
-                [P, KEY_PASSES, P, 4], BF16, tag="e_grouped", name="e_grouped", bufs=3, align_bytes=64
+        def group_e(unit, first, count, bank):
+            nc.scalar.copy(
+                out=e_grouped[unit][:, first : first + count].bitcast(F32),
+                in_=bank.rearrange("p g u q -> p g q u"),
             )
-            for first, count, bank in e_turned[unit]:
-                nc.scalar.copy(
-                    out=e_grouped[unit][:, first : first + count].bitcast(F32),
-                    in_=bank[:].rearrange("p g u q -> p g q u"),
-                )
 
         def quantise_e(unit):
             h, i = divmod(unit, Q_BLOCKS)
             if i == 0:
                 e_words[h] = work.tile(
-                    [P, Q_BLOCKS, KEY_PASSES, P], U32, tag="e_words", name="e_words", align_bytes=64
+                    [P, Q_BLOCKS, KEY_PASSES, P], U32, tag="e_words", name="e_words", bufs=3, align_bytes=64
                 )
                 e_scales[h] = work.tile(
-                    [P, Q_BLOCKS, KEY_PASSES, P], U8, tag="e_scales", name="e_scales", align_bytes=64
+                    [P, Q_BLOCKS, KEY_PASSES, P], U8, tag="e_scales", name="e_scales", bufs=3, align_bytes=64
                 )
             for first, count in ((0, 2), (2, 1)):
                 nc.vector.quantize_mx(
@@ -288,34 +295,39 @@ def tile_flashattentionmodule_pa_kernel(
                     in_=e_grouped[unit][:, first : first + count].rearrange("p g q t -> p (g q t)"),
                 )
 
-        def weighted_values(h):
-            o[h] = other_pool.tile([P, Q_BLOCKS, P], F32, tag="bank", name="o")
-            for i in range(Q_BLOCKS):
+        def weighted_values(h, half):
+            o[(h, half)] = other_pool.tile([P, 2, P], F32, tag="bank", name="o")
+            for j in range(2):
                 for g in range(KEY_PASSES):
                     nc.tensor.matmul_mx(
-                        out=o[h][:, i, :],
-                        lhsT=e_words[h][:, i, g, :].bitcast(FP8X4),
-                        lhsT_scale=e_scales[h][:, i, g, :],
+                        out=o[(h, half)][:, j, :],
+                        lhsT=e_words[h][:, 2 * half + j, g, :].bitcast(FP8X4),
+                        lhsT_scale=e_scales[h][:, 2 * half + j, g, :],
                         rhs=v_words[h][:, g, :].bitcast(FP8X4),
                         rhs_scale=v_scales[h][:, g, :],
                         start=(g == 0),
                         stop=(g == KEY_PASSES - 1),
                     )
 
-        def normalise_and_store(h):
+        def invert_sums(h):
             row_sum = small.tile([P, Q_BLOCKS], F32, tag="row_sum", name="row_sum")
             nc.vector.reduce_sum(out=row_sum[:], in_=sums[h][:], axis=AX.X)
-            inverse = small.tile([P, Q_BLOCKS], F32, tag="inverse", name="inverse")
-            nc.vector.reciprocal(out=inverse[:], in_=row_sum[:])
-            result = work.tile([P, Q_BLOCKS, P], F32, tag="result", name="result")
+            inverse[h] = small.tile([P, Q_BLOCKS], F32, tag="inverse", name="inverse")
+            nc.vector.reciprocal(out=inverse[h][:], in_=row_sum[:])
+            result[h] = work.tile([P, Q_BLOCKS, P], F32, tag="result", name="result")
+
+        def normalise(h, half):
+            blocks = slice(2 * half, 2 * half + 2)
             nc.vector.tensor_tensor(
-                out=result[:],
-                in0=o[h][:],
-                in1=inverse[:].unsqueeze(2).to_broadcast([P, Q_BLOCKS, P]),
+                out=result[h][:, blocks, :],
+                in0=o[(h, half)][:],
+                in1=inverse[h][:, blocks].unsqueeze(2).to_broadcast([P, 2, P]),
                 op=ALU.mult,
             )
+
+        def store(h):
             nc.sync.dma_start(
-                out=out[0].rearrange("(i r) (h d) -> h r i d", r=P, d=P)[h], in_=result[:]
+                out=out[0].rearrange("(i r) (h d) -> h r i d", r=P, d=P)[h], in_=result[h][:]
             )
 
         def is_unit(unit):
@@ -330,47 +342,90 @@ def tile_flashattentionmodule_pa_kernel(
         load_w(0)
         nc.sync.dma_start(out=bias[:], in_=bv.partition_broadcast(P))
         load_head(1)
-        turn_cached_keys(0)
-        turn_new_keys_and_queries(0)
 
-        for now in range(-2, UNITS + Q_BLOCKS):
+        columns[0] = work.tile([P, 2 * PAST], BF16, tag="columns", name="columns")
+        for quarter in QUARTER_ORDER:
+            operand_bank = other_pool.tile([P, 4, P], BF16, tag="bank", name="operand_bank")
+            turn_operands(0, quarter, operand_bank[:])
+            copy_operands(0, quarter, operand_bank[:])
+
+        for now in range(-2, Q_BLOCKS * (HEADS + 1) + 3):
             h, block = divmod(now, Q_BLOCKS)
+            behind = now - 1
+            next_head, piece = divmod(now + 1 + Q_BLOCKS, Q_BLOCKS)
+            quarter = QUARTER_ORDER[piece]
+            turns_operands = 1 <= next_head < HEADS
             refills = [divmod(UNIT_BANKS * now + SCORE_BANKS + n, UNIT_BANKS) for n in range(UNIT_BANKS)]
-            if is_unit(now - 1):
-                turn_e(now - 1)
+
+            if is_unit(behind):
+                e_grouped[behind] = work.tile(
+                    [P, KEY_PASSES, P, 4], BF16, tag="e_grouped", name="e_grouped", bufs=3, align_bytes=64
+                )
+                e_bank = other_pool.tile([P, 2, 2, P], F32, tag="bank", name="e_bank")
+                turn_e(behind, 0, 2, e_bank[:])
+            if is_unit(behind) or turns_operands:
+                shared_bank = other_pool.tile([P, BANK], F32, tag="bank", name="shared_bank")
+                e_half = shared_bank[:, 0 : BANK // 2].rearrange("p (g u q) -> p g u q", g=1, u=2)
+                operand_half = shared_bank[:, BANK // 2 :].bitcast(BF16).rearrange("p (j r) -> p j r", j=4)
+            if is_unit(behind):
+                turn_e(behind, 2, 1, e_half)
+            if turns_operands:
+                if piece == 0:
+                    columns[next_head] = work.tile([P, 2 * PAST], BF16, tag="columns", name="columns")
+                turn_operands(next_head, quarter, operand_half)
+
             if is_unit(now - 2):
                 quantise_e(now - 2)
             if is_unit(now):
                 exponentials(now)
-            if is_unit(now - 1):
-                group_e(now - 1)
+            if is_unit(behind):
+                group_e(behind, 0, 2, e_bank[:])
+                group_e(behind, 2, 1, e_half)
+            if turns_operands:
+                copy_operands(next_head, quarter, operand_half)
+
             if is_unit(refills[0][0]):
                 score_bank(*refills[0])
-
-            if block == 0 and is_head(h) and is_head(h + 1):
-                turn_cached_keys(h + 1)
-            if block == 1 and is_head(h) and is_head(h + 1):
-                turn_new_keys_and_queries(h + 1)
-            if block == 2 and is_head(h - 1):
-                project_new_values(h - 1)
-            if block == 3 and h == 0:
-                quantise_x()
+            if block == 0 and is_head(h - 2):
+                weighted_values(h - 2, 0)
+            if block == 1 and is_head(h - 1):
+                project_new_values(h - 1, 0)
+            if block == 2 and is_head(h - 2):
+                weighted_values(h - 2, 1)
             if block == 3 and is_head(h - 1):
-                weighted_values(h - 1)
-
+                project_new_values(h - 1, 1)
+            if 1 <= now <= X_PASSES:
+                turn_x(now - 1)
             for unit, c in refills[1:]:
                 if is_unit(unit):
                     score_bank(unit, c)
+
             if is_unit(now + 1):
                 row_maximum(now + 1)
+            if 1 <= now <= X_PASSES:
+                quantise_x(now - 1)
+            if block == 0:
+                if is_head(h - 1):
+                    quantise_cached_values(h - 1)
+                if is_head(h - 2):
+                    invert_sums(h - 2)
+                    normalise(h - 2, 0)
+            if block == 1:
+                if is_head(h):
+                    group_cached_values(h, 0)
+                if is_head(h - 1):
+                    group_new_values(h - 1, 0)
+            if block == 2 and is_head(h - 2):
+                normalise(h - 2, 1)
+                store(h - 2)
+            if block == 3:
+                if is_head(h):
+                    group_cached_values(h, 1)
+                if is_head(h - 1):
+                    group_new_values(h - 1, 1)
+                    quantise_new_values(h - 1)
 
-            if block == 0 and is_head(h):
-                quantise_cached_values(h)
-                if is_head(h + 2):
-                    if (h + 2) % HEADS_PER_W_LOAD == 0:
-                        load_w((h + 2) // HEADS_PER_W_LOAD)
-                    load_head(h + 2)
-            if block == 2 and is_head(h - 1):
-                quantise_new_values(h - 1)
-            if block == 3 and is_head(h - 1):
-                normalise_and_store(h - 1)
+            if block == 0 and is_head(h) and is_head(h + 2):
+                if (h + 2) % HEADS_PER_W_LOAD == 0:
+                    load_w((h + 2) // HEADS_PER_W_LOAD)
+                load_head(h + 2)

@@ -89,7 +89,8 @@ def tile_flashattentionmodule_pa_kernel(
         x_grouped = {}
         y, o = {}, {}
         score_banks = {}
-        shift = {}
+        bank_max, cached_shift, shift = {}, {}, {}
+        row_sum = {}
         e_grouped = {}
 
         def load_head(h):
@@ -235,20 +236,32 @@ def tile_flashattentionmodule_pa_kernel(
                 )
             score_banks[(unit, c)] = (s, width)
 
-        def row_maximum(unit):
-            bank_max = small.tile([P, UNIT_BANKS], F32, tag="bank_max", name="bank_max")
-            for c in range(2):
-                s, width = score_banks[(unit, c)]
-                nc.vector.reduce_max(out=bank_max[:, c : c + 1], in_=s[:, 0:width], axis=AX.X)
-            cached = small.tile([P, 1], F32, tag="cached", name="cached")
+        def bank_maximum(unit, c):
+            if c == 0:
+                bank_max[unit] = small.tile([P, UNIT_BANKS], F32, tag="bank_max", name="bank_max")
+            s, width = score_banks[(unit, c)]
+            nc.vector.reduce_max(out=bank_max[unit][:, c : c + 1], in_=s[:, 0:width], axis=AX.X)
+
+        def join_cached_maxima(unit):
+            cached_shift[unit] = small.tile([P, 1], F32, tag="cached_shift", name="cached_shift")
             nc.vector.tensor_scalar(
-                out=cached[:], in0=bank_max[:, 0:1], scalar1=bank_max[:, 1:2], scalar2=-SCALE, op0=ALU.max, op1=ALU.mult
+                out=cached_shift[unit][:],
+                in0=bank_max[unit][:, 0:1],
+                scalar1=bank_max[unit][:, 1:2],
+                scalar2=-SCALE,
+                op0=ALU.max,
+                op1=ALU.mult,
             )
-            s, width = score_banks[(unit, 2)]
-            nc.vector.reduce_max(out=bank_max[:, 2:3], in_=s[:, 0:width], axis=AX.X)
+
+        def join_all_maxima(unit):
             shift[unit] = small.tile([P, 1], F32, tag="shift", name="shift")
             nc.vector.tensor_scalar(
-                out=shift[unit][:], in0=bank_max[:, 2:3], scalar1=-SCALE, scalar2=cached[:], op0=ALU.mult, op1=ALU.min
+                out=shift[unit][:],
+                in0=bank_max[unit][:, 2:3],
+                scalar1=-SCALE,
+                scalar2=cached_shift[unit][:],
+                op0=ALU.mult,
+                op1=ALU.min,
             )
 
         def exponentials(unit):
@@ -279,21 +292,20 @@ def tile_flashattentionmodule_pa_kernel(
                 in_=bank.rearrange("p g u q -> p g q u"),
             )
 
-        def quantise_e(unit):
+        def quantise_e(unit, first, count):
             h, i = divmod(unit, Q_BLOCKS)
-            if i == 0:
+            if i == 0 and first == 0:
                 e_words[h] = work.tile(
                     [P, Q_BLOCKS, KEY_PASSES, P], U32, tag="e_words", name="e_words", bufs=3, align_bytes=64
                 )
                 e_scales[h] = work.tile(
                     [P, Q_BLOCKS, KEY_PASSES, P], U8, tag="e_scales", name="e_scales", bufs=3, align_bytes=64
                 )
-            for first, count in ((0, 2), (2, 1)):
-                nc.vector.quantize_mx(
-                    out=e_words[h][:, i, first : first + count, :].rearrange("p g q -> p (g q)").bitcast(FP8X4),
-                    scales=e_scales[h][:, i, first : first + count, :].rearrange("p g q -> p (g q)"),
-                    in_=e_grouped[unit][:, first : first + count].rearrange("p g q t -> p (g q t)"),
-                )
+            nc.vector.quantize_mx(
+                out=e_words[h][:, i, first : first + count, :].rearrange("p g q -> p (g q)").bitcast(FP8X4),
+                scales=e_scales[h][:, i, first : first + count, :].rearrange("p g q -> p (g q)"),
+                in_=e_grouped[unit][:, first : first + count].rearrange("p g q t -> p (g q t)"),
+            )
 
         def weighted_values(h, half):
             o[(h, half)] = other_pool.tile([P, 2, P], F32, tag="bank", name="o")
@@ -309,11 +321,13 @@ def tile_flashattentionmodule_pa_kernel(
                         stop=(g == KEY_PASSES - 1),
                     )
 
+        def add_sums(h):
+            row_sum[h] = small.tile([P, Q_BLOCKS], F32, tag="row_sum", name="row_sum")
+            nc.vector.reduce_sum(out=row_sum[h][:], in_=sums[h][:], axis=AX.X)
+
         def invert_sums(h):
-            row_sum = small.tile([P, Q_BLOCKS], F32, tag="row_sum", name="row_sum")
-            nc.vector.reduce_sum(out=row_sum[:], in_=sums[h][:], axis=AX.X)
             inverse[h] = small.tile([P, Q_BLOCKS], F32, tag="inverse", name="inverse")
-            nc.vector.reciprocal(out=inverse[h][:], in_=row_sum[:])
+            nc.vector.reciprocal(out=inverse[h][:], in_=row_sum[h][:])
             result[h] = work.tile([P, Q_BLOCKS, P], F32, tag="result", name="result")
 
         def normalise(h, half):
@@ -374,8 +388,6 @@ def tile_flashattentionmodule_pa_kernel(
                     columns[next_head] = work.tile([P, 2 * PAST], BF16, tag="columns", name="columns")
                 turn_operands(next_head, quarter, operand_half)
 
-            if is_unit(now - 2):
-                quantise_e(now - 2)
             if is_unit(now):
                 exponentials(now)
             if is_unit(behind):
@@ -400,30 +412,44 @@ def tile_flashattentionmodule_pa_kernel(
                 if is_unit(unit):
                     score_bank(unit, c)
 
-            if is_unit(now + 1):
-                row_maximum(now + 1)
+            ahead = now + 1
+            if is_unit(ahead):
+                bank_maximum(ahead, 0)
+                bank_maximum(ahead, 1)
+            if is_unit(now - 2):
+                quantise_e(now - 2, 0, 2)
+            if is_unit(ahead):
+                join_cached_maxima(ahead)
+                bank_maximum(ahead, 2)
+            if is_unit(now - 2):
+                quantise_e(now - 2, 2, 1)
+            if is_unit(ahead):
+                join_all_maxima(ahead)
             if 1 <= now <= X_PASSES:
                 quantise_x(now - 1)
             if block == 0:
+                if is_head(h - 2):
+                    invert_sums(h - 2)
                 if is_head(h - 1):
                     quantise_cached_values(h - 1)
                 if is_head(h - 2):
-                    invert_sums(h - 2)
                     normalise(h - 2, 0)
             if block == 1:
-                if is_head(h):
-                    group_cached_values(h, 0)
                 if is_head(h - 1):
                     group_new_values(h - 1, 0)
+                if is_head(h):
+                    group_cached_values(h, 0)
             if block == 2 and is_head(h - 2):
                 normalise(h - 2, 1)
                 store(h - 2)
             if block == 3:
+                if is_head(h - 1):
+                    group_new_values(h - 1, 1)
                 if is_head(h):
                     group_cached_values(h, 1)
                 if is_head(h - 1):
-                    group_new_values(h - 1, 1)
                     quantise_new_values(h - 1)
+                    add_sums(h - 1)
 
             if block == 0 and is_head(h) and is_head(h + 2):
                 if (h + 2) % HEADS_PER_W_LOAD == 0:

@@ -93,7 +93,7 @@ def tile_flashattentionmodule_pa_kernel(
         row_sum = {}
         e_grouped = {}
 
-        def load_head(h):
+        def load_keys_and_queries(h):
             k_past[h] = raw.tile([P, 2, 4, P], BF16, tag="k_past", name="k_past")
             nc.sync.dma_start(
                 out=k_past[h][:], in_=past_k[0, h].rearrange("(a r c) d -> r a c d", a=2, c=4)
@@ -102,6 +102,8 @@ def tile_flashattentionmodule_pa_kernel(
             nc.sync.dma_start(out=q_rows[h][:], in_=q[0, h].rearrange("(i r) d -> r i d", r=P))
             k_fresh[h] = raw.tile([P, Q_BLOCKS, P], BF16, tag="k_fresh", name="k_fresh")
             nc.sync.dma_start(out=k_fresh[h][:], in_=k_new[0, h].rearrange("(j r) d -> r j d", r=P))
+
+        def load_cached_values(h):
             v_past[h] = raw.tile([P, 8, P], BF16, tag="v_past", name="v_past")
             nc.sync.dma_start(out=v_past[h][:], in_=past_v[0, h].rearrange("(p j) d -> p j d", j=8))
 
@@ -237,7 +239,7 @@ def tile_flashattentionmodule_pa_kernel(
             score_banks[(unit, c)] = (s, width)
 
         def bank_maximum(unit, c):
-            if c == 0:
+            if unit not in bank_max:
                 bank_max[unit] = small.tile([P, UNIT_BANKS], F32, tag="bank_max", name="bank_max")
             s, width = score_banks[(unit, c)]
             nc.vector.reduce_max(out=bank_max[unit][:, c : c + 1], in_=s[:, 0:width], axis=AX.X)
@@ -294,7 +296,7 @@ def tile_flashattentionmodule_pa_kernel(
 
         def quantise_e(unit, first, count):
             h, i = divmod(unit, Q_BLOCKS)
-            if i == 0 and first == 0:
+            if h not in e_words:
                 e_words[h] = work.tile(
                     [P, Q_BLOCKS, KEY_PASSES, P], U32, tag="e_words", name="e_words", bufs=3, align_bytes=64
                 )
@@ -350,12 +352,14 @@ def tile_flashattentionmodule_pa_kernel(
         def is_head(h):
             return 0 <= h < HEADS
 
-        load_head(0)
+        load_keys_and_queries(0)
+        load_keys_and_queries(1)
         load_x()
+        load_cached_values(0)
         load_w_scales()
         load_w(0)
         nc.sync.dma_start(out=bias[:], in_=bv.partition_broadcast(P))
-        load_head(1)
+        load_cached_values(1)
 
         columns[0] = work.tile([P, 2 * PAST], BF16, tag="columns", name="columns")
         for quarter in QUARTER_ORDER:
@@ -390,11 +394,11 @@ def tile_flashattentionmodule_pa_kernel(
 
             if is_unit(now):
                 exponentials(now)
+            if turns_operands:
+                copy_operands(next_head, quarter, operand_half)
             if is_unit(behind):
                 group_e(behind, 0, 2, e_bank[:])
                 group_e(behind, 2, 1, e_half)
-            if turns_operands:
-                copy_operands(next_head, quarter, operand_half)
 
             if is_unit(refills[0][0]):
                 score_bank(*refills[0])
@@ -414,17 +418,16 @@ def tile_flashattentionmodule_pa_kernel(
 
             ahead = now + 1
             if is_unit(ahead):
-                bank_maximum(ahead, 0)
                 bank_maximum(ahead, 1)
-            if is_unit(now - 2):
-                quantise_e(now - 2, 0, 2)
-            if is_unit(ahead):
-                join_cached_maxima(ahead)
+                bank_maximum(ahead, 0)
                 bank_maximum(ahead, 2)
+                join_cached_maxima(ahead)
             if is_unit(now - 2):
                 quantise_e(now - 2, 2, 1)
             if is_unit(ahead):
                 join_all_maxima(ahead)
+            if is_unit(now - 2):
+                quantise_e(now - 2, 0, 2)
             if 1 <= now <= X_PASSES:
                 quantise_x(now - 1)
             if block == 0:
@@ -454,4 +457,5 @@ def tile_flashattentionmodule_pa_kernel(
             if block == 0 and is_head(h) and is_head(h + 2):
                 if (h + 2) % HEADS_PER_W_LOAD == 0:
                     load_w((h + 2) // HEADS_PER_W_LOAD)
-                load_head(h + 2)
+                load_keys_and_queries(h + 2)
+                load_cached_values(h + 2)

@@ -94,12 +94,12 @@ def tile_flashattentionmodule_pa_kernel(
         e_grouped = {}
 
         def load_keys_and_queries(h):
+            q_rows[h] = raw.tile([P, Q_BLOCKS, P], BF16, tag="q_rows", name="q_rows")
+            nc.sync.dma_start(out=q_rows[h][:], in_=q[0, h].rearrange("(i r) d -> r i d", r=P))
             k_past[h] = raw.tile([P, 2, 4, P], BF16, tag="k_past", name="k_past")
             nc.sync.dma_start(
                 out=k_past[h][:], in_=past_k[0, h].rearrange("(a r c) d -> r a c d", a=2, c=4)
             )
-            q_rows[h] = raw.tile([P, Q_BLOCKS, P], BF16, tag="q_rows", name="q_rows")
-            nc.sync.dma_start(out=q_rows[h][:], in_=q[0, h].rearrange("(i r) d -> r i d", r=P))
             k_fresh[h] = raw.tile([P, Q_BLOCKS, P], BF16, tag="k_fresh", name="k_fresh")
             nc.sync.dma_start(out=k_fresh[h][:], in_=k_new[0, h].rearrange("(j r) d -> r j d", r=P))
 
@@ -377,7 +377,7 @@ def tile_flashattentionmodule_pa_kernel(
 
             if is_unit(behind):
                 e_grouped[behind] = work.tile(
-                    [P, KEY_PASSES, P, 4], BF16, tag="e_grouped", name="e_grouped", bufs=3, align_bytes=64
+                    [P, KEY_PASSES, P, 4], BF16, tag="e_grouped", name="e_grouped", bufs=4, align_bytes=64
                 )
                 e_bank = other_pool.tile([P, 2, 2, P], F32, tag="bank", name="e_bank")
                 turn_e(behind, 0, 2, e_bank[:])
@@ -420,14 +420,15 @@ def tile_flashattentionmodule_pa_kernel(
             if is_unit(ahead):
                 bank_maximum(ahead, 1)
                 bank_maximum(ahead, 0)
-                bank_maximum(ahead, 2)
+            if is_unit(now - 3):
+                quantise_e(now - 3, 0, 2)
+            if is_unit(ahead):
                 join_cached_maxima(ahead)
-            if is_unit(now - 2):
-                quantise_e(now - 2, 2, 1)
+                bank_maximum(ahead, 2)
+            if is_unit(now - 3):
+                quantise_e(now - 3, 2, 1)
             if is_unit(ahead):
                 join_all_maxima(ahead)
-            if is_unit(now - 2):
-                quantise_e(now - 2, 0, 2)
             if 1 <= now <= X_PASSES:
                 quantise_x(now - 1)
             if block == 0:

@@ -421,12 +421,12 @@ def tile_flashattentionmodule_pa_kernel(
                 bank_maximum(ahead, 1)
                 bank_maximum(ahead, 0)
             if is_unit(now - 3):
-                quantise_e(now - 3, 0, 2)
-            if is_unit(ahead):
-                join_cached_maxima(ahead)
-                bank_maximum(ahead, 2)
-            if is_unit(now - 3):
                 quantise_e(now - 3, 2, 1)
+            if is_unit(ahead):
+                bank_maximum(ahead, 2)
+                join_cached_maxima(ahead)
+            if is_unit(now - 3):
+                quantise_e(now - 3, 0, 2)
             if is_unit(ahead):
                 join_all_maxima(ahead)
             if 1 <= now <= X_PASSES:

@@ -175,8 +175,8 @@ def tile_flashattentionmodule_pa_kernel(
                     [P, KEY_PASSES, P, 4], BF16, tag="v_grouped", name="v_grouped", align_bytes=64
                 )
             nc.vector.tensor_copy(
-                out=v_grouped[h][:, g].rearrange("p d (u c) -> p d u c", u=2),
-                in_=v_past[h][:].rearrange("p (c g u) d -> p g d u c", c=2, g=2)[:, g],
+                out=v_grouped[h][:, g].rearrange("p (n i) (u c) -> p n u c i", i=4, u=2),
+                in_=v_past[h][:].rearrange("p (c g u) (n i) -> p g n u c i", c=2, g=2, i=4)[:, g],
             )
 
         def quantise_cached_values(h):

@@ -46,7 +46,7 @@ def tile_flashattentionmodule_pa_kernel(
         work = ctx.enter_context(tc.tile_pool(name="work", bufs=2))
         small = ctx.enter_context(tc.tile_pool(name="small", bufs=4))
         score_pool = ctx.enter_context(tc.psum_pool(name="score_pool", bufs=SCORE_BANKS))
-        other_pool = ctx.enter_context(tc.psum_pool(name="other_pool", bufs=8 - SCORE_BANKS))
+        other_pool = ctx.enter_context(tc.psum_pool(name="other_pool", bufs=1))
 
         ident_bf = const.tile([P, P], BF16, name="ident_bf")
         make_identity(nc, ident_bf[:])
@@ -130,7 +130,7 @@ def tile_flashattentionmodule_pa_kernel(
         def turn_x(g):
             x_grouped[g] = work.tile([P, NEW, 4], BF16, tag="x_grouped", name="x_grouped", align_bytes=64)
             for half in range(2):
-                bank = other_pool.tile([P, 2, 2, P], F32, tag="bank", name="x_bank")
+                bank = other_pool.tile([P, 2, 2, P], F32, tag=("mx_bank", "e_bank")[half], name="x_bank")
                 for part in range(2):
                     pairs = x_rows[:, 2 * half + part, :].bitcast(F32)
                     for u in range(2):
@@ -189,13 +189,16 @@ def tile_flashattentionmodule_pa_kernel(
             )
 
         def project_new_values(h, u):
-            y[(h, u)] = other_pool.tile([P, 2, P], F32, tag="bank", name="y")
+            if u == 0 and h == HEADS - 1:
+                y[h] = score_pool.tile([P, 4, P], F32, tag="s", name="y_last")
+            elif u == 0:
+                y[h] = other_pool.tile([P, 4, P], F32, tag="mx_bank", name="y")
             cols = slice(P * h, P * (h + 1))
             for c in range(2):
                 tokens = slice(P * (2 * u + c), P * (2 * u + c + 1))
                 for g in range(X_PASSES):
                     nc.tensor.matmul_mx(
-                        out=y[(h, u)][:, c, :],
+                        out=y[h][:, 2 * u + c, :],
                         lhsT=x_words[:, g, tokens].bitcast(FP8X4),
                         lhsT_scale=x_scales[:, g, tokens],
                         rhs=w_words[:, g, cols].bitcast(FP8X4),
@@ -204,11 +207,11 @@ def tile_flashattentionmodule_pa_kernel(
                         stop=(g == X_PASSES - 1),
                     )
 
-        def group_new_values(h, u):
+        def group_new_values(h):
             nc.vector.tensor_tensor(
-                out=v_grouped[h][:, 2, :, 2 * u : 2 * u + 2],
-                in0=y[(h, u)][:].rearrange("p c d -> p d c"),
-                in1=bias[:, P * h : P * (h + 1)].unsqueeze(2).to_broadcast([P, P, 2]),
+                out=v_grouped[h][:, 2],
+                in0=y[h][:].rearrange("p t d -> p d t"),
+                in1=bias[:, P * h : P * (h + 1)].unsqueeze(2).to_broadcast([P, P, 4]),
                 op=ALU.add,
             )
 
@@ -310,11 +313,12 @@ def tile_flashattentionmodule_pa_kernel(
             )
 
         def weighted_values(h, half):
-            o[(h, half)] = other_pool.tile([P, 2, P], F32, tag="bank", name="o")
+            if half == 0:
+                o[h] = other_pool.tile([P, Q_BLOCKS, P], F32, tag="mx_bank", name="o")
             for j in range(2):
                 for g in range(KEY_PASSES):
                     nc.tensor.matmul_mx(
-                        out=o[(h, half)][:, j, :],
+                        out=o[h][:, 2 * half + j, :],
                         lhsT=e_words[h][:, 2 * half + j, g, :].bitcast(FP8X4),
                         lhsT_scale=e_scales[h][:, 2 * half + j, g, :],
                         rhs=v_words[h][:, g, :].bitcast(FP8X4),
@@ -330,14 +334,13 @@ def tile_flashattentionmodule_pa_kernel(
         def invert_sums(h):
             inverse[h] = small.tile([P, Q_BLOCKS], F32, tag="inverse", name="inverse")
             nc.vector.reciprocal(out=inverse[h][:], in_=row_sum[h][:])
-            result[h] = work.tile([P, Q_BLOCKS, P], F32, tag="result", name="result")
 
-        def normalise(h, half):
-            blocks = slice(2 * half, 2 * half + 2)
+        def normalise(h):
+            result[h] = work.tile([P, Q_BLOCKS, P], F32, tag="result", name="result")
             nc.vector.tensor_tensor(
-                out=result[h][:, blocks, :],
-                in0=o[(h, half)][:],
-                in1=inverse[h][:, blocks].unsqueeze(2).to_broadcast([P, 2, P]),
+                out=result[h][:],
+                in0=o[h][:],
+                in1=inverse[h][:].unsqueeze(2).to_broadcast([P, Q_BLOCKS, P]),
                 op=ALU.mult,
             )
 
@@ -363,11 +366,17 @@ def tile_flashattentionmodule_pa_kernel(
 
         columns[0] = work.tile([P, 2 * PAST], BF16, tag="columns", name="columns")
         for quarter in QUARTER_ORDER:
-            operand_bank = other_pool.tile([P, 4, P], BF16, tag="bank", name="operand_bank")
+            operand_bank = other_pool.tile(
+                [P, 4, P], BF16, tag=("e_bank", "shared_bank", "mx_bank")[quarter % 3], name="operand_bank"
+            )
             turn_operands(0, quarter, operand_bank[:])
             copy_operands(0, quarter, operand_bank[:])
 
-        for now in range(-2, Q_BLOCKS * (HEADS + 1) + 3):
+        def head_at(now, offset):
+            j, rest = divmod(now - offset, Q_BLOCKS)
+            return j if rest == 0 and is_head(j) else -1
+
+        for now in range(-2, UNITS + 4):
             h, block = divmod(now, Q_BLOCKS)
             behind = now - 1
             next_head, piece = divmod(now + 1 + Q_BLOCKS, Q_BLOCKS)
@@ -375,14 +384,20 @@ def tile_flashattentionmodule_pa_kernel(
             turns_operands = 1 <= next_head < HEADS
             refills = [divmod(UNIT_BANKS * now + SCORE_BANKS + n, UNIT_BANKS) for n in range(UNIT_BANKS)]
 
+            if block == 0 and is_head(h) and is_head(h + 2):
+                if (h + 2) % HEADS_PER_W_LOAD == 0:
+                    load_w((h + 2) // HEADS_PER_W_LOAD)
+                load_keys_and_queries(h + 2)
+                load_cached_values(h + 2)
+
             if is_unit(behind):
                 e_grouped[behind] = work.tile(
                     [P, KEY_PASSES, P, 4], BF16, tag="e_grouped", name="e_grouped", bufs=4, align_bytes=64
                 )
-                e_bank = other_pool.tile([P, 2, 2, P], F32, tag="bank", name="e_bank")
+                e_bank = other_pool.tile([P, 2, 2, P], F32, tag="e_bank", name="e_bank")
                 turn_e(behind, 0, 2, e_bank[:])
             if is_unit(behind) or turns_operands:
-                shared_bank = other_pool.tile([P, BANK], F32, tag="bank", name="shared_bank")
+                shared_bank = other_pool.tile([P, BANK], F32, tag="shared_bank", name="shared_bank")
                 e_half = shared_bank[:, 0 : BANK // 2].rearrange("p (g u q) -> p g u q", g=1, u=2)
                 operand_half = shared_bank[:, BANK // 2 :].bitcast(BF16).rearrange("p (j r) -> p j r", j=4)
             if is_unit(behind):
@@ -402,14 +417,22 @@ def tile_flashattentionmodule_pa_kernel(
 
             if is_unit(refills[0][0]):
                 score_bank(*refills[0])
-            if block == 0 and is_head(h - 2):
-                weighted_values(h - 2, 0)
-            if block == 1 and is_head(h - 1):
-                project_new_values(h - 1, 0)
-            if block == 2 and is_head(h - 2):
-                weighted_values(h - 2, 1)
-            if block == 3 and is_head(h - 1):
-                project_new_values(h - 1, 1)
+            if 0 <= head_at(now, 5) < HEADS - 1:
+                project_new_values(head_at(now, 5), 0)
+            if 0 <= head_at(now, 6) < HEADS - 1:
+                project_new_values(head_at(now, 6), 1)
+            if 0 <= head_at(now, 7) < HEADS - 1:
+                weighted_values(head_at(now, 7), 0)
+            if 0 <= head_at(now, 8) < HEADS - 1:
+                weighted_values(head_at(now, 8), 1)
+            if now == UNITS - 2:
+                project_new_values(HEADS - 1, 0)
+            if now == UNITS - 1:
+                project_new_values(HEADS - 1, 1)
+            if now == UNITS + 1:
+                weighted_values(HEADS - 1, 0)
+            if now == UNITS + 3:
+                weighted_values(HEADS - 1, 1)
             if 1 <= now <= X_PASSES:
                 turn_x(now - 1)
             for unit, c in refills[1:]:
@@ -419,6 +442,7 @@ def tile_flashattentionmodule_pa_kernel(
             ahead = now + 1
             if is_unit(ahead):
                 bank_maximum(ahead, 1)
+            if is_unit(ahead):
                 bank_maximum(ahead, 0)
             if is_unit(now - 3):
                 quantise_e(now - 3, 2, 1)
@@ -427,36 +451,33 @@ def tile_flashattentionmodule_pa_kernel(
                 join_cached_maxima(ahead)
             if is_unit(now - 3):
                 quantise_e(now - 3, 0, 2)
+            if 0 <= head_at(now, 7) < HEADS - 1:
+                invert_sums(head_at(now, 7))
+            if now == UNITS + 2:
+                invert_sums(HEADS - 1)
             if is_unit(ahead):
                 join_all_maxima(ahead)
             if 1 <= now <= X_PASSES:
                 quantise_x(now - 1)
-            if block == 0:
-                if is_head(h - 2):
-                    invert_sums(h - 2)
-                if is_head(h - 1):
-                    quantise_cached_values(h - 1)
-                if is_head(h - 2):
-                    normalise(h - 2, 0)
-            if block == 1:
-                if is_head(h - 1):
-                    group_new_values(h - 1, 0)
-                if is_head(h):
-                    group_cached_values(h, 0)
-            if block == 2 and is_head(h - 2):
-                normalise(h - 2, 1)
-                store(h - 2)
-            if block == 3:
-                if is_head(h - 1):
-                    group_new_values(h - 1, 1)
-                if is_head(h):
-                    group_cached_values(h, 1)
-                if is_head(h - 1):
-                    quantise_new_values(h - 1)
-                    add_sums(h - 1)
-
-            if block == 0 and is_head(h) and is_head(h + 2):
-                if (h + 2) % HEADS_PER_W_LOAD == 0:
-                    load_w((h + 2) // HEADS_PER_W_LOAD)
-                load_keys_and_queries(h + 2)
-                load_cached_values(h + 2)
+            if head_at(now, 4) >= 0:
+                quantise_cached_values(head_at(now, 4))
+            if 0 <= head_at(now, 8) < HEADS - 1:
+                normalise(head_at(now, 8))
+                store(head_at(now, 8))
+            if now == UNITS + 3:
+                normalise(HEADS - 1)
+                store(HEADS - 1)
+            if head_at(now, 5) >= 0:
+                add_sums(head_at(now, 5))
+            if head_at(now, 1) >= 0:
+                group_cached_values(head_at(now, 1), 0)
+            if 0 <= head_at(now, 6) < HEADS - 1:
+                group_new_values(head_at(now, 6))
+            if now == UNITS - 1:
+                group_new_values(HEADS - 1)
+            if head_at(now, 2) >= 0:
+                group_cached_values(head_at(now, 2), 1)
+            if 0 <= head_at(now, 6) < HEADS - 1:
+                quantise_new_values(head_at(now, 6))
+            if now == UNITS:
+                quantise_new_values(HEADS - 1)

@@ -30,6 +30,7 @@ UNIT_BANKS = 3
 SCORE_BANKS = 5
 QUARTER_ORDER = (3, 0, 1, 2)
 SCALE = 1.0 / math.sqrt(P)
+VALUE_LEAD = 3
 MASKED = -1.0e10
 
 FLOPS = 2 * NEW * FEATURES * FEATURES + 2 * 2 * HEADS * NEW * (PAST + NEW) * P
@@ -104,7 +105,7 @@ def tile_flashattentionmodule_pa_kernel(
             nc.sync.dma_start(out=k_fresh[h][:], in_=k_new[0, h].rearrange("(j r) d -> r j d", r=P))
 
         def load_cached_values(h):
-            v_past[h] = raw.tile([P, 8, P], BF16, tag="v_past", name="v_past")
+            v_past[h] = raw.tile([P, 8, P], BF16, tag="v_past", name="v_past", bufs=VALUE_LEAD + 2)
             nc.sync.dma_start(out=v_past[h][:], in_=past_v[0, h].rearrange("(p j) d -> p j d", j=8))
 
         def load_x():
@@ -172,7 +173,7 @@ def tile_flashattentionmodule_pa_kernel(
         def group_cached_values(h, g):
             if g == 0:
                 v_grouped[h] = work.tile(
-                    [P, KEY_PASSES, P, 4], BF16, tag="v_grouped", name="v_grouped", align_bytes=64
+                    [P, KEY_PASSES, P, 4], BF16, tag="v_grouped", name="v_grouped", bufs=VALUE_LEAD + 3, align_bytes=64
                 )
             nc.vector.tensor_copy(
                 out=v_grouped[h][:, g].rearrange("p (n i) (u c) -> p n u c i", i=4, u=2),
@@ -180,8 +181,12 @@ def tile_flashattentionmodule_pa_kernel(
             )
 
         def quantise_cached_values(h):
-            v_words[h] = work.tile([P, KEY_PASSES, P], U32, tag="v_words", name="v_words", align_bytes=64)
-            v_scales[h] = work.tile([P, KEY_PASSES, P], U8, tag="v_scales", name="v_scales", align_bytes=64)
+            v_words[h] = work.tile(
+                [P, KEY_PASSES, P], U32, tag="v_words", name="v_words", bufs=VALUE_LEAD + 3, align_bytes=64
+            )
+            v_scales[h] = work.tile(
+                [P, KEY_PASSES, P], U8, tag="v_scales", name="v_scales", bufs=VALUE_LEAD + 3, align_bytes=64
+            )
             nc.vector.quantize_mx(
                 out=v_words[h][:, 0:2, :].rearrange("p g d -> p (g d)").bitcast(FP8X4),
                 scales=v_scales[h][:, 0:2, :].rearrange("p g d -> p (g d)"),
@@ -388,7 +393,10 @@ def tile_flashattentionmodule_pa_kernel(
                 if (h + 2) % HEADS_PER_W_LOAD == 0:
                     load_w((h + 2) // HEADS_PER_W_LOAD)
                 load_keys_and_queries(h + 2)
-                load_cached_values(h + 2)
+            if block == 0 and is_head(h):
+                for late in range(2 if h == 0 else h + VALUE_LEAD + 1, h + VALUE_LEAD + 2):
+                    if is_head(late):
+                        load_cached_values(late)
 
             if is_unit(behind):
                 e_grouped[behind] = work.tile(
@@ -457,10 +465,15 @@ def tile_flashattentionmodule_pa_kernel(
                 invert_sums(HEADS - 1)
             if is_unit(ahead):
                 join_all_maxima(ahead)
+            if 1 <= now <= VALUE_LEAD + 1:
+                group_cached_values(now - 1, 0)
+                group_cached_values(now - 1, 1)
             if 1 <= now <= X_PASSES:
                 quantise_x(now - 1)
-            if head_at(now, 4) >= 0:
-                quantise_cached_values(head_at(now, 4))
+            if 1 <= now <= VALUE_LEAD + 1:
+                quantise_cached_values(now - 1)
+            if head_at(now, 4) >= 0 and is_head(head_at(now, 4) + VALUE_LEAD) and head_at(now, 4) >= 1:
+                quantise_cached_values(head_at(now, 4) + VALUE_LEAD)
             if 0 <= head_at(now, 8) < HEADS - 1:
                 normalise(head_at(now, 8))
                 store(head_at(now, 8))
@@ -469,14 +482,14 @@ def tile_flashattentionmodule_pa_kernel(
                 store(HEADS - 1)
             if head_at(now, 5) >= 0:
                 add_sums(head_at(now, 5))
-            if head_at(now, 1) >= 0:
-                group_cached_values(head_at(now, 1), 0)
+            if head_at(now, 1) >= 1 and is_head(head_at(now, 1) + VALUE_LEAD):
+                group_cached_values(head_at(now, 1) + VALUE_LEAD, 0)
             if 0 <= head_at(now, 6) < HEADS - 1:
                 group_new_values(head_at(now, 6))
             if now == UNITS - 1:
                 group_new_values(HEADS - 1)
-            if head_at(now, 2) >= 0:
-                group_cached_values(head_at(now, 2), 1)
+            if head_at(now, 2) >= 1 and is_head(head_at(now, 2) + VALUE_LEAD):
+                group_cached_values(head_at(now, 2) + VALUE_LEAD, 1)
             if 0 <= head_at(now, 6) < HEADS - 1:
                 quantise_new_values(head_at(now, 6))
             if now == UNITS:

@@ -31,6 +31,8 @@ SCORE_BANKS = 5
 QUARTER_ORDER = (3, 0, 1, 2)
 SCALE = 1.0 / math.sqrt(P)
 VALUE_LEAD = 3
+LAST = HEADS - 1
+E_PARTS = ((0, 2048), (2048, 2048), (4096, 1024), (5120, 1024))
 MASKED = -1.0e10
 
 FLOPS = 2 * NEW * FEATURES * FEATURES + 2 * 2 * HEADS * NEW * (PAST + NEW) * P
@@ -77,7 +79,10 @@ def tile_flashattentionmodule_pa_kernel(
                 nc.vector.memset(e_tile[:, PAST + P * (i + 1) :], 0.0)
             e_tiles.append(e_tile)
 
-        x_rows = const.tile([P, 4, FEATURES], BF16, name="x_rows")
+        x_rows = []
+        for g in range(X_PASSES):
+            x_slice = const.tile([P, 4, K_PASS], BF16, name="x_rows%d" % g)
+            x_rows.append(x_slice)
         x_words = const.tile([P, X_PASSES, NEW], U32, name="x_words", align_bytes=64)
         x_scales = const.tile([P, X_PASSES, NEW], U8, name="x_scales", align_bytes=64)
         w_words = const.tile([P, X_PASSES, FEATURES], U32, name="w_words", align_bytes=64)
@@ -108,11 +113,12 @@ def tile_flashattentionmodule_pa_kernel(
             v_past[h] = raw.tile([P, 8, P], BF16, tag="v_past", name="v_past", bufs=VALUE_LEAD + 2)
             nc.sync.dma_start(out=v_past[h][:], in_=past_v[0, h].rearrange("(p j) d -> p j d", j=8))
 
-        def load_x():
-            by_part = x[0].rearrange("(u m c) k -> u c m k", u=2, c=2)
+        def load_x(g):
+            by_part = x[0].rearrange("(u m c) k -> u m c k", u=2, c=2)
             for u in range(2):
-                for c in range(2):
-                    nc.sync.dma_start(out=x_rows[:, 2 * u + c, :], in_=by_part[u, c])
+                nc.sync.dma_start(
+                    out=x_rows[g][:, 2 * u : 2 * u + 2, :], in_=by_part[u][:, :, K_PASS * g : K_PASS * (g + 1)]
+                )
 
         def load_w_scales():
             for quadrant in range(4):
@@ -133,11 +139,9 @@ def tile_flashattentionmodule_pa_kernel(
             for half in range(2):
                 bank = other_pool.tile([P, 2, 2, P], F32, tag=("mx_bank", "e_bank")[half], name="x_bank")
                 for part in range(2):
-                    pairs = x_rows[:, 2 * half + part, :].bitcast(F32)
+                    pairs = x_rows[g][:, 2 * half + part, :].bitcast(F32)
                     for u in range(2):
-                        nc.tensor.transpose(
-                            bank[:, part, u, :], pairs[:, 256 * g + u : 256 * (g + 1) : 2], ident_f32[:]
-                        )
+                        nc.tensor.transpose(bank[:, part, u, :], pairs[:, u : K_PASS // 2 : 2], ident_f32[:])
                 nc.scalar.copy(
                     out=x_grouped[g][:, 256 * half : 256 * (half + 1), :]
                     .bitcast(F32)
@@ -164,8 +168,9 @@ def tile_flashattentionmodule_pa_kernel(
             for j in range(4):
                 nc.tensor.transpose(half_bank[:, j, :], operand_rows(h, 4 * quarter + j), ident_bf[:])
 
-        def copy_operands(h, quarter, half_bank):
-            nc.scalar.copy(
+        def copy_operands(h, quarter, half_bank, on_vector=False):
+            copy = nc.vector.tensor_copy if on_vector else nc.scalar.copy
+            copy(
                 out=columns[h][:, BANK * quarter : BANK * (quarter + 1)],
                 in_=half_bank.rearrange("p j r -> p (j r)"),
             )
@@ -297,13 +302,15 @@ def tile_flashattentionmodule_pa_kernel(
                     nc.tensor.transpose(bank[:, g, u, :], pairs[:, left : left + P], ident_f32[:])
 
         def group_e(unit, first, count, bank):
+            h, i = divmod(unit, Q_BLOCKS)
             nc.scalar.copy(
-                out=e_grouped[unit][:, first : first + count].bitcast(F32),
+                out=e_grouped[h][:, i, first : first + count].bitcast(F32),
                 in_=bank.rearrange("p g u q -> p g q u"),
             )
 
-        def quantise_e(unit, first, count):
-            h, i = divmod(unit, Q_BLOCKS)
+        def quantise_e(h, part):
+            left, width = E_PARTS[part]
+            words = slice(left // 4, (left + width) // 4)
             if h not in e_words:
                 e_words[h] = work.tile(
                     [P, Q_BLOCKS, KEY_PASSES, P], U32, tag="e_words", name="e_words", bufs=3, align_bytes=64
@@ -312,25 +319,28 @@ def tile_flashattentionmodule_pa_kernel(
                     [P, Q_BLOCKS, KEY_PASSES, P], U8, tag="e_scales", name="e_scales", bufs=3, align_bytes=64
                 )
             nc.vector.quantize_mx(
-                out=e_words[h][:, i, first : first + count, :].rearrange("p g q -> p (g q)").bitcast(FP8X4),
-                scales=e_scales[h][:, i, first : first + count, :].rearrange("p g q -> p (g q)"),
-                in_=e_grouped[unit][:, first : first + count].rearrange("p g q t -> p (g q t)"),
+                out=e_words[h][:].rearrange("p i g q -> p (i g q)")[:, words].bitcast(FP8X4),
+                scales=e_scales[h][:].rearrange("p i g q -> p (i g q)")[:, words],
+                in_=e_grouped[h][:].rearrange("p i g q t -> p (i g q t)")[:, left : left + width],
             )
+
+        def weighted_block(h, i, sums_out):
+            for g in range(KEY_PASSES):
+                nc.tensor.matmul_mx(
+                    out=sums_out,
+                    lhsT=e_words[h][:, i, g, :].bitcast(FP8X4),
+                    lhsT_scale=e_scales[h][:, i, g, :],
+                    rhs=v_words[h][:, g, :].bitcast(FP8X4),
+                    rhs_scale=v_scales[h][:, g, :],
+                    start=(g == 0),
+                    stop=(g == KEY_PASSES - 1),
+                )
 
         def weighted_values(h, half):
             if half == 0:
                 o[h] = other_pool.tile([P, Q_BLOCKS, P], F32, tag="mx_bank", name="o")
-            for j in range(2):
-                for g in range(KEY_PASSES):
-                    nc.tensor.matmul_mx(
-                        out=o[h][:, 2 * half + j, :],
-                        lhsT=e_words[h][:, 2 * half + j, g, :].bitcast(FP8X4),
-                        lhsT_scale=e_scales[h][:, 2 * half + j, g, :],
-                        rhs=v_words[h][:, g, :].bitcast(FP8X4),
-                        rhs_scale=v_scales[h][:, g, :],
-                        start=(g == 0),
-                        stop=(g == KEY_PASSES - 1),
-                    )
+            for i in (2 * half, 2 * half + 1):
+                weighted_block(h, i, o[h][:, i, :])
 
         def add_sums(h):
             row_sum[h] = small.tile([P, Q_BLOCKS], F32, tag="row_sum", name="row_sum")
@@ -349,9 +359,19 @@ def tile_flashattentionmodule_pa_kernel(
                 op=ALU.mult,
             )
 
-        def store(h):
+        def normalise_on_scalar(h, first, count, sums_in, quotient):
+            for n in range(count):
+                nc.scalar.activation(
+                    out=quotient[:, n, :],
+                    in_=sums_in[:, n, :],
+                    func=ACT.Copy,
+                    scale=inverse[h][:, first + n : first + n + 1],
+                )
+
+        def store(h, first=0, count=Q_BLOCKS, quotient=None):
             nc.sync.dma_start(
-                out=out[0].rearrange("(i r) (h d) -> h r i d", r=P, d=P)[h], in_=result[h][:]
+                out=out[0].rearrange("(i r) (h d) -> h r i d", r=P, d=P)[h][:, first : first + count, :],
+                in_=(result[h] if quotient is None else quotient)[:],
             )
 
         def is_unit(unit):
@@ -362,7 +382,8 @@ def tile_flashattentionmodule_pa_kernel(
 
         load_keys_and_queries(0)
         load_keys_and_queries(1)
-        load_x()
+        for g in range(X_PASSES):
+            load_x(g)
         load_cached_values(0)
         load_w_scales()
         load_w(0)
@@ -370,20 +391,28 @@ def tile_flashattentionmodule_pa_kernel(
         load_cached_values(1)
 
         columns[0] = work.tile([P, 2 * PAST], BF16, tag="columns", name="columns")
-        for quarter in QUARTER_ORDER:
-            operand_bank = other_pool.tile(
-                [P, 4, P], BF16, tag=("e_bank", "shared_bank", "mx_bank")[quarter % 3], name="operand_bank"
-            )
+        for n, quarter in enumerate(QUARTER_ORDER):
+            if n < 3:
+                operand_bank = other_pool.tile(
+                    [P, 4, P], BF16, tag=("e_bank", "shared_bank", "mx_bank")[n], name="operand_bank"
+                )
+            else:
+                operand_bank = score_pool.tile([P, 4, P], BF16, tag="s", name="operand_bank")
             turn_operands(0, quarter, operand_bank[:])
-            copy_operands(0, quarter, operand_bank[:])
+            copy_operands(0, quarter, operand_bank[:], on_vector=(n % 2 == 1))
 
         def head_at(now, offset):
             j, rest = divmod(now - offset, Q_BLOCKS)
             return j if rest == 0 and is_head(j) else -1
 
-        for now in range(-2, UNITS + 4):
+        def ahead_of(now, offset):
+            j = head_at(now, offset)
+            return j + VALUE_LEAD if j >= 1 and is_head(j + VALUE_LEAD) else -1
+
+        for now in range(-2, UNITS):
             h, block = divmod(now, Q_BLOCKS)
             behind = now - 1
+            ahead = now + 1
             next_head, piece = divmod(now + 1 + Q_BLOCKS, Q_BLOCKS)
             quarter = QUARTER_ORDER[piece]
             turns_operands = 1 <= next_head < HEADS
@@ -399,9 +428,10 @@ def tile_flashattentionmodule_pa_kernel(
                         load_cached_values(late)
 
             if is_unit(behind):
-                e_grouped[behind] = work.tile(
-                    [P, KEY_PASSES, P, 4], BF16, tag="e_grouped", name="e_grouped", bufs=4, align_bytes=64
-                )
+                if behind % Q_BLOCKS == 0:
+                    e_grouped[behind // Q_BLOCKS] = work.tile(
+                        [P, Q_BLOCKS, KEY_PASSES, P, 4], BF16, tag="e_grouped", name="e_grouped", align_bytes=64
+                    )
                 e_bank = other_pool.tile([P, 2, 2, P], F32, tag="e_bank", name="e_bank")
                 turn_e(behind, 0, 2, e_bank[:])
             if is_unit(behind) or turns_operands:
@@ -425,72 +455,97 @@ def tile_flashattentionmodule_pa_kernel(
 
             if is_unit(refills[0][0]):
                 score_bank(*refills[0])
-            if 0 <= head_at(now, 5) < HEADS - 1:
+            if 0 <= head_at(now, 5) < LAST:
                 project_new_values(head_at(now, 5), 0)
-            if 0 <= head_at(now, 6) < HEADS - 1:
+            if 0 <= head_at(now, 6) < LAST:
                 project_new_values(head_at(now, 6), 1)
-            if 0 <= head_at(now, 7) < HEADS - 1:
+            if 0 <= head_at(now, 7) < LAST - 1:
                 weighted_values(head_at(now, 7), 0)
-            if 0 <= head_at(now, 8) < HEADS - 1:
+            if 0 <= head_at(now, 8) < LAST - 1:
                 weighted_values(head_at(now, 8), 1)
             if now == UNITS - 2:
-                project_new_values(HEADS - 1, 0)
+                project_new_values(LAST, 0)
             if now == UNITS - 1:
-                project_new_values(HEADS - 1, 1)
-            if now == UNITS + 1:
-                weighted_values(HEADS - 1, 0)
-            if now == UNITS + 3:
-                weighted_values(HEADS - 1, 1)
-            if 1 <= now <= X_PASSES:
-                turn_x(now - 1)
+                project_new_values(LAST, 1)
+            if 0 <= now < X_PASSES:
+                turn_x(now)
             for unit, c in refills[1:]:
                 if is_unit(unit):
                     score_bank(unit, c)
 
-            ahead = now + 1
             if is_unit(ahead):
-                bank_maximum(ahead, 1)
-            if is_unit(ahead):
-                bank_maximum(ahead, 0)
-            if is_unit(now - 3):
-                quantise_e(now - 3, 2, 1)
+                bank_maximum(ahead, 0 if ahead == 0 else 1)
+                bank_maximum(ahead, 1 if ahead == 0 else 0)
             if is_unit(ahead):
                 bank_maximum(ahead, 2)
                 join_cached_maxima(ahead)
-            if is_unit(now - 3):
-                quantise_e(now - 3, 0, 2)
-            if 0 <= head_at(now, 7) < HEADS - 1:
+            if ahead_of(now, 4) >= 0:
+                quantise_cached_values(ahead_of(now, 4))
+            if ahead_of(now, 1) >= 0:
+                group_cached_values(ahead_of(now, 1), 0)
+            if head_at(now, 6) >= 0:
+                quantise_e(head_at(now, 6), 2)
+            if ahead_of(now, 3) >= 0:
+                group_cached_values(ahead_of(now, 3), 1)
+            if head_at(now, 7) >= 0:
                 invert_sums(head_at(now, 7))
-            if now == UNITS + 2:
-                invert_sums(HEADS - 1)
             if is_unit(ahead):
                 join_all_maxima(ahead)
+            if 1 <= now <= X_PASSES:
+                quantise_x(now - 1)
+            if 2 <= now <= VALUE_LEAD + 2:
+                quantise_cached_values(now - 2)
+            if head_at(now, 3) >= 0:
+                quantise_e(head_at(now, 3), 0)
+            if head_at(now, 5) >= 0:
+                quantise_e(head_at(now, 5), 1)
             if 1 <= now <= VALUE_LEAD + 1:
                 group_cached_values(now - 1, 0)
                 group_cached_values(now - 1, 1)
-            if 1 <= now <= X_PASSES:
-                quantise_x(now - 1)
-            if 1 <= now <= VALUE_LEAD + 1:
-                quantise_cached_values(now - 1)
-            if head_at(now, 4) >= 0 and is_head(head_at(now, 4) + VALUE_LEAD) and head_at(now, 4) >= 1:
-                quantise_cached_values(head_at(now, 4) + VALUE_LEAD)
-            if 0 <= head_at(now, 8) < HEADS - 1:
+            if head_at(now, 8) >= 0:
                 normalise(head_at(now, 8))
                 store(head_at(now, 8))
-            if now == UNITS + 3:
-                normalise(HEADS - 1)
-                store(HEADS - 1)
             if head_at(now, 5) >= 0:
                 add_sums(head_at(now, 5))
-            if head_at(now, 1) >= 1 and is_head(head_at(now, 1) + VALUE_LEAD):
-                group_cached_values(head_at(now, 1) + VALUE_LEAD, 0)
-            if 0 <= head_at(now, 6) < HEADS - 1:
+            if head_at(now, 6) >= 0:
                 group_new_values(head_at(now, 6))
-            if now == UNITS - 1:
-                group_new_values(HEADS - 1)
-            if head_at(now, 2) >= 1 and is_head(head_at(now, 2) + VALUE_LEAD):
-                group_cached_values(head_at(now, 2) + VALUE_LEAD, 1)
-            if 0 <= head_at(now, 6) < HEADS - 1:
+                quantise_e(head_at(now, 6), 3)
                 quantise_new_values(head_at(now, 6))
-            if now == UNITS:
-                quantise_new_values(HEADS - 1)
+            if now == UNITS - 1:
+                group_new_values(LAST)
+
+        end_bank = score_pool.tile([P, 2, 2, P], F32, tag="s", name="end_bank")
+        turn_e(UNITS - 1, 0, 2, end_bank[:])
+        end_half = score_pool.tile([P, 1, 2, P], F32, tag="s", name="end_half")
+        turn_e(UNITS - 1, 2, 1, end_half[:])
+        group_e(UNITS - 1, 0, 2, end_bank[:])
+        group_e(UNITS - 1, 2, 1, end_half[:])
+        weighted_values(LAST - 1, 0)
+        weighted_values(LAST - 1, 1)
+        result[LAST - 1] = work.tile([P, Q_BLOCKS, P], F32, tag="result", name="result")
+        normalise_on_scalar(LAST - 1, 0, Q_BLOCKS, o[LAST - 1], result[LAST - 1])
+        store(LAST - 1)
+
+        quantise_e(LAST, 1)
+        quantise_new_values(LAST)
+        quantise_e(LAST, 2)
+        add_sums(LAST)
+        quantise_e(LAST, 3)
+        invert_sums(LAST)
+        o_first = score_pool.tile([P, Q_BLOCKS - 1, P], F32, tag="s", name="o_first")
+        for i in range(Q_BLOCKS - 1):
+            weighted_block(LAST, i, o_first[:, i, :])
+        o_last = score_pool.tile([P, 1, P], F32, tag="s", name="o_last")
+        weighted_block(LAST, Q_BLOCKS - 1, o_last[:, 0, :])
+        result_first = work.tile([P, Q_BLOCKS - 1, P], F32, tag="result", name="result_first")
+        normalise_on_scalar(LAST, 0, Q_BLOCKS - 1, o_first, result_first)
+        store(LAST, 0, Q_BLOCKS - 1, result_first)
+        result_last = work.tile([P, 1, P], F32, tag="result_last", name="result_last")
+        nc.vector.tensor_scalar(
+            out=result_last[:, 0, :],
+            in0=o_last[:, 0, :],
+            scalar1=inverse[LAST][:, Q_BLOCKS - 1 : Q_BLOCKS],
+            scalar2=None,
+            op0=ALU.mult,
+        )
+        store(LAST, Q_BLOCKS - 1, 1, result_last)

@@ -33,6 +33,7 @@ SCALE = 1.0 / math.sqrt(P)
 VALUE_LEAD = 3
 LAST = HEADS - 1
 E_PARTS = ((0, 2048), (2048, 2048), (4096, 1024), (5120, 1024))
+LOWEST = -3.0e38
 MASKED = -1.0e10
 
 FLOPS = 2 * NEW * FEATURES * FEATURES + 2 * 2 * HEADS * NEW * (PAST + NEW) * P
@@ -69,6 +70,10 @@ def tile_flashattentionmodule_pa_kernel(
         causal = const.tile([P, P], BF16, name="causal")
         nc.vector.tensor_copy(out=causal[:], in_=causal_f32[:])
 
+        join_factors = const.tile([P, UNIT_BANKS], F32, name="join_factors")
+        nc.vector.memset(join_factors[:, 0 : UNIT_BANKS - 1], 1.0)
+        nc.vector.memset(join_factors[:, UNIT_BANKS - 1 :], -SCALE)
+
         w_scales = const.tile([P, FEATURES], U8, name="w_scales", align_bytes=64)
         nc.vector.memset(w_scales[:].bitcast(I32), 0)
 
@@ -95,7 +100,7 @@ def tile_flashattentionmodule_pa_kernel(
         x_grouped = {}
         y, o = {}, {}
         score_banks = {}
-        bank_max, cached_shift, shift = {}, {}, {}
+        bank_max, shift = {}, {}
         row_sum = {}
         e_grouped = {}
 
@@ -257,27 +262,17 @@ def tile_flashattentionmodule_pa_kernel(
             s, width = score_banks[(unit, c)]
             nc.vector.reduce_max(out=bank_max[unit][:, c : c + 1], in_=s[:, 0:width], axis=AX.X)
 
-        def join_cached_maxima(unit):
-            cached_shift[unit] = small.tile([P, 1], F32, tag="cached_shift", name="cached_shift")
-            nc.vector.tensor_scalar(
-                out=cached_shift[unit][:],
-                in0=bank_max[unit][:, 0:1],
-                scalar1=bank_max[unit][:, 1:2],
-                scalar2=-SCALE,
+        def join_maxima(unit):
+            joined = small.tile([P, UNIT_BANKS], F32, tag="joined", name="joined")
+            nc.vector.tensor_tensor_scan(
+                out=joined[:],
+                data0=bank_max[unit][:],
+                data1=join_factors[:],
+                initial=LOWEST,
                 op0=ALU.max,
                 op1=ALU.mult,
             )
-
-        def join_all_maxima(unit):
-            shift[unit] = small.tile([P, 1], F32, tag="shift", name="shift")
-            nc.vector.tensor_scalar(
-                out=shift[unit][:],
-                in0=bank_max[unit][:, 2:3],
-                scalar1=-SCALE,
-                scalar2=cached_shift[unit][:],
-                op0=ALU.mult,
-                op1=ALU.min,
-            )
+            shift[unit] = joined[:, UNIT_BANKS - 1 : UNIT_BANKS]
 
         def exponentials(unit):
             h, i = divmod(unit, Q_BLOCKS)
@@ -289,7 +284,7 @@ def tile_flashattentionmodule_pa_kernel(
                     out=e_tiles[i][:, BANK * c : BANK * c + width],
                     in_=s[:, 0:width],
                     func=ACT.Exp,
-                    bias=shift[unit][:],
+                    bias=shift[unit],
                     scale=SCALE,
                     accum_out=sums[h][:, i, c : c + 1],
                 )
@@ -478,7 +473,6 @@ def tile_flashattentionmodule_pa_kernel(
                 bank_maximum(ahead, 1 if ahead == 0 else 0)
             if is_unit(ahead):
                 bank_maximum(ahead, 2)
-                join_cached_maxima(ahead)
             if ahead_of(now, 4) >= 0:
                 quantise_cached_values(ahead_of(now, 4))
             if ahead_of(now, 1) >= 0:
@@ -490,7 +484,7 @@ def tile_flashattentionmodule_pa_kernel(
             if head_at(now, 7) >= 0:
                 invert_sums(head_at(now, 7))
             if is_unit(ahead):
-                join_all_maxima(ahead)
+                join_maxima(ahead)
             if 1 <= now <= X_PASSES:
                 quantise_x(now - 1)
             if 2 <= now <= VALUE_LEAD + 2:

@@ -29,10 +29,12 @@ UNITS = HEADS * Q_BLOCKS
 UNIT_BANKS = 3
 SCORE_BANKS = 5
 QUARTER_ORDER = (3, 0, 1, 2)
+QUARTER_PAIRS = ((0, 3), (1, 2))
 SCALE = 1.0 / math.sqrt(P)
-VALUE_LEAD = 3
+VALUE_LEAD = 1
 LAST = HEADS - 1
 E_PARTS = ((0, 2048), (2048, 2048), (4096, 1024), (5120, 1024))
+LAST_E_PARTS = ((0, 2048), (2048, 2048), (4096, 512), (4608, 1024), (5632, 512))
 LOWEST = -3.0e38
 MASKED = -1.0e10
 
@@ -97,7 +99,7 @@ def tile_flashattentionmodule_pa_kernel(
         columns = {}
         v_grouped, v_words, v_scales = {}, {}, {}
         e_words, e_scales, sums, inverse, result = {}, {}, {}, {}, {}
-        x_grouped = {}
+        x_banks, x_grouped = {}, {}
         y, o = {}, {}
         score_banks = {}
         bank_max, shift = {}, {}
@@ -139,20 +141,23 @@ def tile_flashattentionmodule_pa_kernel(
                 in_=Wv_words.rearrange("g p n t -> p g (n t)").bitcast(I32)[:, :, cols],
             )
 
-        def turn_x(g):
-            x_grouped[g] = work.tile([P, NEW, 4], BF16, tag="x_grouped", name="x_grouped", align_bytes=64)
-            for half in range(2):
-                bank = other_pool.tile([P, 2, 2, P], F32, tag=("mx_bank", "e_bank")[half], name="x_bank")
-                for part in range(2):
-                    pairs = x_rows[g][:, 2 * half + part, :].bitcast(F32)
-                    for u in range(2):
-                        nc.tensor.transpose(bank[:, part, u, :], pairs[:, u : K_PASS // 2 : 2], ident_f32[:])
-                nc.scalar.copy(
-                    out=x_grouped[g][:, 256 * half : 256 * (half + 1), :]
-                    .bitcast(F32)
-                    .rearrange("p (part m) u -> p part m u", part=2),
-                    in_=bank[:].rearrange("p part u m -> p part m u"),
-                )
+        def turn_x(g, half):
+            if half == 0:
+                x_grouped[g] = work.tile([P, NEW, 4], BF16, tag="x_grouped", name="x_grouped", align_bytes=64)
+            bank = other_pool.tile([P, 2, 2, P], F32, tag="mx_bank", name="x_bank")
+            for part in range(2):
+                pairs = x_rows[g][:, 2 * half + part, :].bitcast(F32)
+                for u in range(2):
+                    nc.tensor.transpose(bank[:, part, u, :], pairs[:, u : K_PASS // 2 : 2], ident_f32[:])
+            x_banks[(g, half)] = bank
+
+        def group_x(g, half, copy):
+            copy(
+                out=x_grouped[g][:, 256 * half : 256 * (half + 1), :]
+                .bitcast(F32)
+                .rearrange("p (part m) u -> p part m u", part=2),
+                in_=x_banks[(g, half)][:].rearrange("p part u m -> p part m u"),
+            )
 
         def quantise_x(g):
             nc.vector.quantize_mx(
@@ -178,6 +183,12 @@ def tile_flashattentionmodule_pa_kernel(
             copy(
                 out=columns[h][:, BANK * quarter : BANK * (quarter + 1)],
                 in_=half_bank.rearrange("p j r -> p (j r)"),
+            )
+
+        def copy_operand_pair(h, pair, bank):
+            nc.scalar.copy(
+                out=columns[h][:].rearrange("p (a c) -> p a c", a=4)[:, pair[0] : pair[1] + 1 : pair[1] - pair[0]],
+                in_=bank[:].rearrange("p n j r -> p n (j r)"),
             )
 
         def group_cached_values(h, g):
@@ -303,8 +314,15 @@ def tile_flashattentionmodule_pa_kernel(
                 in_=bank.rearrange("p g u q -> p g q u"),
             )
 
+        def group_third_passes(unit, bank):
+            h, i = divmod(unit, Q_BLOCKS)
+            nc.scalar.copy(
+                out=e_grouped[h][:, i - 1 : i + 1, 2].bitcast(F32),
+                in_=bank[:].rearrange("p n u q -> p n q u"),
+            )
+
         def quantise_e(h, part):
-            left, width = E_PARTS[part]
+            left, width = (LAST_E_PARTS if h == LAST else E_PARTS)[part]
             words = slice(left // 4, (left + width) // 4)
             if h not in e_words:
                 e_words[h] = work.tile(
@@ -345,14 +363,17 @@ def tile_flashattentionmodule_pa_kernel(
             inverse[h] = small.tile([P, Q_BLOCKS], F32, tag="inverse", name="inverse")
             nc.vector.reciprocal(out=inverse[h][:], in_=row_sum[h][:])
 
-        def normalise(h):
-            result[h] = work.tile([P, Q_BLOCKS, P], F32, tag="result", name="result")
+        def divide(h, first, count, sums_in, quotient):
             nc.vector.tensor_tensor(
-                out=result[h][:],
-                in0=o[h][:],
-                in1=inverse[h][:].unsqueeze(2).to_broadcast([P, Q_BLOCKS, P]),
+                out=quotient[:],
+                in0=sums_in[:],
+                in1=inverse[h][:, first : first + count].unsqueeze(2).to_broadcast([P, count, P]),
                 op=ALU.mult,
             )
+
+        def normalise(h):
+            result[h] = work.tile([P, Q_BLOCKS, P], F32, tag="result", name="result")
+            divide(h, 0, Q_BLOCKS, o[h], result[h])
 
         def normalise_on_scalar(h, first, count, sums_in, quotient):
             for n in range(count):
@@ -404,13 +425,12 @@ def tile_flashattentionmodule_pa_kernel(
             j = head_at(now, offset)
             return j + VALUE_LEAD if j >= 1 and is_head(j + VALUE_LEAD) else -1
 
-        for now in range(-2, UNITS):
+        for now in range(-2, UNITS - 1):
             h, block = divmod(now, Q_BLOCKS)
             behind = now - 1
             ahead = now + 1
             next_head, piece = divmod(now + 1 + Q_BLOCKS, Q_BLOCKS)
-            quarter = QUARTER_ORDER[piece]
-            turns_operands = 1 <= next_head < HEADS
+            turns_operands = 1 <= next_head < HEADS and piece % 2 == 0
             refills = [divmod(UNIT_BANKS * now + SCORE_BANKS + n, UNIT_BANKS) for n in range(UNIT_BANKS)]
 
             if block == 0 and is_head(h) and is_head(h + 2):
@@ -429,27 +449,31 @@ def tile_flashattentionmodule_pa_kernel(
                     )
                 e_bank = other_pool.tile([P, 2, 2, P], F32, tag="e_bank", name="e_bank")
                 turn_e(behind, 0, 2, e_bank[:])
-            if is_unit(behind) or turns_operands:
-                shared_bank = other_pool.tile([P, BANK], F32, tag="shared_bank", name="shared_bank")
-                e_half = shared_bank[:, 0 : BANK // 2].rearrange("p (g u q) -> p g u q", g=1, u=2)
-                operand_half = shared_bank[:, BANK // 2 :].bitcast(BF16).rearrange("p (j r) -> p j r", j=4)
-            if is_unit(behind):
-                turn_e(behind, 2, 1, e_half)
+            if is_unit(behind) and behind % 2 == 1:
+                third_bank = other_pool.tile([P, 2, 2, P], F32, tag="shared_bank", name="third_bank")
+                turn_e(behind - 1, 2, 1, third_bank[:, 0:1])
+                turn_e(behind, 2, 1, third_bank[:, 1:2])
             if turns_operands:
                 if piece == 0:
                     columns[next_head] = work.tile([P, 2 * PAST], BF16, tag="columns", name="columns")
-                turn_operands(next_head, quarter, operand_half)
+                pair = QUARTER_PAIRS[piece // 2]
+                pair_bank = other_pool.tile([P, 2, 4, P], BF16, tag="shared_bank", name="pair_bank")
+                for n in range(2):
+                    turn_operands(next_head, pair[n], pair_bank[:, n])
 
             if is_unit(now):
                 exponentials(now)
             if turns_operands:
-                copy_operands(next_head, quarter, operand_half)
+                copy_operand_pair(next_head, pair, pair_bank)
             if is_unit(behind):
                 group_e(behind, 0, 2, e_bank[:])
-                group_e(behind, 2, 1, e_half)
+            if is_unit(behind) and behind % 2 == 1:
+                group_third_passes(behind, third_bank)
 
             if is_unit(refills[0][0]):
                 score_bank(*refills[0])
+            if 0 <= now < X_PASSES:
+                turn_x(now, 0)
             if 0 <= head_at(now, 5) < LAST:
                 project_new_values(head_at(now, 5), 0)
             if 0 <= head_at(now, 6) < LAST:
@@ -460,10 +484,10 @@ def tile_flashattentionmodule_pa_kernel(
                 weighted_values(head_at(now, 8), 1)
             if now == UNITS - 2:
                 project_new_values(LAST, 0)
-            if now == UNITS - 1:
                 project_new_values(LAST, 1)
             if 0 <= now < X_PASSES:
-                turn_x(now)
+                turn_x(now, 1)
+                group_x(now, 1, nc.scalar.copy)
             for unit, c in refills[1:]:
                 if is_unit(unit):
                     score_bank(unit, c)
@@ -483,6 +507,8 @@ def tile_flashattentionmodule_pa_kernel(
                 group_cached_values(ahead_of(now, 3), 1)
             if head_at(now, 7) >= 0:
                 invert_sums(head_at(now, 7))
+            if 0 <= now < X_PASSES:
+                group_x(now, 0, nc.vector.tensor_copy)
             if is_unit(ahead):
                 join_maxima(ahead)
             if 1 <= now <= X_PASSES:
@@ -505,41 +531,46 @@ def tile_flashattentionmodule_pa_kernel(
                 group_new_values(head_at(now, 6))
                 quantise_e(head_at(now, 6), 3)
                 quantise_new_values(head_at(now, 6))
-            if now == UNITS - 1:
-                group_new_values(LAST)
 
-        end_bank = score_pool.tile([P, 2, 2, P], F32, tag="s", name="end_bank")
-        turn_e(UNITS - 1, 0, 2, end_bank[:])
-        end_half = score_pool.tile([P, 1, 2, P], F32, tag="s", name="end_half")
-        turn_e(UNITS - 1, 2, 1, end_half[:])
-        group_e(UNITS - 1, 0, 2, end_bank[:])
-        group_e(UNITS - 1, 2, 1, end_half[:])
+        before = UNITS - 2
+        last = UNITS - 1
+        e_bank = other_pool.tile([P, 2, 2, P], F32, tag="e_bank", name="e_bank")
+        turn_e(before, 0, 2, e_bank[:])
+        third_before = other_pool.tile([P, 1, 2, P], F32, tag="shared_bank", name="third_before")
+        turn_e(before, 2, 1, third_before[:])
+
+        exponentials(last)
+
+        invert_sums(LAST - 1)
+        quantise_e(LAST, 0)
+        group_new_values(LAST)
+
+        e_last = score_pool.tile([P, 2, 2, P], F32, tag="s", name="e_last")
+        turn_e(last, 0, 2, e_last[:])
+        third_last = score_pool.tile([P, 1, 2, P], F32, tag="s", name="third_last")
+        turn_e(last, 2, 1, third_last[:])
         weighted_values(LAST - 1, 0)
         weighted_values(LAST - 1, 1)
+        group_e(before, 0, 2, e_bank[:])
+        group_e(before, 2, 1, third_before[:])
+        group_e(last, 0, 2, e_last[:])
+        group_e(last, 2, 1, third_last[:])
         result[LAST - 1] = work.tile([P, Q_BLOCKS, P], F32, tag="result", name="result")
         normalise_on_scalar(LAST - 1, 0, Q_BLOCKS, o[LAST - 1], result[LAST - 1])
         store(LAST - 1)
 
-        quantise_e(LAST, 1)
         quantise_new_values(LAST)
-        quantise_e(LAST, 2)
+        quantise_e(LAST, 1)
         add_sums(LAST)
+        quantise_e(LAST, 2)
         quantise_e(LAST, 3)
         invert_sums(LAST)
-        o_first = score_pool.tile([P, Q_BLOCKS - 1, P], F32, tag="s", name="o_first")
-        for i in range(Q_BLOCKS - 1):
-            weighted_block(LAST, i, o_first[:, i, :])
-        o_last = score_pool.tile([P, 1, P], F32, tag="s", name="o_last")
-        weighted_block(LAST, Q_BLOCKS - 1, o_last[:, 0, :])
-        result_first = work.tile([P, Q_BLOCKS - 1, P], F32, tag="result", name="result_first")
-        normalise_on_scalar(LAST, 0, Q_BLOCKS - 1, o_first, result_first)
-        store(LAST, 0, Q_BLOCKS - 1, result_first)
-        result_last = work.tile([P, 1, P], F32, tag="result_last", name="result_last")
-        nc.vector.tensor_scalar(
-            out=result_last[:, 0, :],
-            in0=o_last[:, 0, :],
-            scalar1=inverse[LAST][:, Q_BLOCKS - 1 : Q_BLOCKS],
-            scalar2=None,
-            op0=ALU.mult,
-        )
-        store(LAST, Q_BLOCKS - 1, 1, result_last)
+        quantise_e(LAST, 4)
+
+        for first, count in ((0, 2), (2, 1), (3, 1)):
+            sums_in = score_pool.tile([P, count, P], F32, tag="s", name="o_part")
+            for n in range(count):
+                weighted_block(LAST, first + n, sums_in[:, n, :])
+            quotient = work.tile([P, count, P], F32, tag="result_%d" % first, name="quotient")
+            divide(LAST, first, count, sums_in, quotient)
+            store(LAST, first, count, quotient)

@@ -51,7 +51,8 @@ def tile_flashattentionmodule_pa_kernel(
         raw = ctx.enter_context(tc.tile_pool(name="raw", bufs=3))
         work = ctx.enter_context(tc.tile_pool(name="work", bufs=2))
         small = ctx.enter_context(tc.tile_pool(name="small", bufs=4))
-        score_pool = ctx.enter_context(tc.psum_pool(name="score_pool", bufs=SCORE_BANKS))
+        score_pool = ctx.enter_context(tc.psum_pool(name="score_pool", bufs=SCORE_BANKS - 1))
+        new_score_pool = ctx.enter_context(tc.psum_pool(name="new_score_pool", bufs=1))
         other_pool = ctx.enter_context(tc.psum_pool(name="other_pool", bufs=1))
 
         ident_bf = const.tile([P, P], BF16, name="ident_bf")
@@ -251,7 +252,10 @@ def tile_flashattentionmodule_pa_kernel(
         def score_bank(unit, c):
             h, i = divmod(unit, Q_BLOCKS)
             queries = columns[h][:, PAST + NEW + P * i : PAST + NEW + P * (i + 1)]
-            s = score_pool.tile([P, BANK], F32, tag="s", name="s")
+            if c < PAST // BANK:
+                s = score_pool.tile([P, BANK], F32, tag="s", name="s")
+            else:
+                s = new_score_pool.tile([P, BANK], F32, tag="s_new", name="s_new")
             if c < PAST // BANK:
                 width = BANK
                 nc.tensor.matmul(
@@ -289,7 +293,7 @@ def tile_flashattentionmodule_pa_kernel(
             h, i = divmod(unit, Q_BLOCKS)
             if i == 0:
                 sums[h] = small.tile([P, Q_BLOCKS, UNIT_BANKS], F32, tag="sums", name="sums")
-            for c in range(UNIT_BANKS):
+            for c in (2, 0, 1):
                 s, width = score_banks[(unit, c)]
                 nc.scalar.activation(
                     out=e_tiles[i][:, BANK * c : BANK * c + width],
@@ -463,13 +467,12 @@ def tile_flashattentionmodule_pa_kernel(
 
             if is_unit(now):
                 exponentials(now)
-            if turns_operands:
-                copy_operand_pair(next_head, pair, pair_bank)
             if is_unit(behind):
                 group_e(behind, 0, 2, e_bank[:])
+            if turns_operands:
+                copy_operand_pair(next_head, pair, pair_bank)
             if is_unit(behind) and behind % 2 == 1:
                 group_third_passes(behind, third_bank)
-
             if is_unit(refills[0][0]):
                 score_bank(*refills[0])
             if 0 <= now < X_PASSES:
@@ -488,10 +491,10 @@ def tile_flashattentionmodule_pa_kernel(
             if 0 <= now < X_PASSES:
                 turn_x(now, 1)
                 group_x(now, 1, nc.scalar.copy)
-            for unit, c in refills[1:]:
-                if is_unit(unit):
-                    score_bank(unit, c)
-
+            if is_unit(refills[1][0]):
+                score_bank(*refills[1])
+            if is_unit(refills[2][0]):
+                score_bank(*refills[2])
             if is_unit(ahead):
                 bank_maximum(ahead, 0 if ahead == 0 else 1)
                 bank_maximum(ahead, 1 if ahead == 0 else 0)

@@ -24,7 +24,7 @@ K_PASS = 512
 Q_BLOCKS = NEW // P
 KEY_PASSES = (PAST + NEW) // K_PASS
 X_PASSES = FEATURES // K_PASS
-HEADS_PER_W_LOAD = 4
+HEADS_PER_W_LOAD = 2
 UNITS = HEADS * Q_BLOCKS
 UNIT_BANKS = 3
 SCORE_BANKS = 5
@@ -48,7 +48,7 @@ def tile_flashattentionmodule_pa_kernel(
     with ExitStack() as ctx:
         ctx.enter_context(tc.manual_schedule())
         const = ctx.enter_context(tc.tile_pool(name="const", bufs=1))
-        raw = ctx.enter_context(tc.tile_pool(name="raw", bufs=3))
+        raw = ctx.enter_context(tc.tile_pool(name="raw", bufs=4))
         work = ctx.enter_context(tc.tile_pool(name="work", bufs=2))
         small = ctx.enter_context(tc.tile_pool(name="small", bufs=4))
         score_pool = ctx.enter_context(tc.psum_pool(name="score_pool", bufs=SCORE_BANKS - 1))
@@ -134,6 +134,10 @@ def tile_flashattentionmodule_pa_kernel(
                     out=w_scales[32 * quadrant : 32 * quadrant + 16, :].bitcast(I32),
                     in_=Wv_scales[:, 4 * quadrant : 4 * quadrant + 4, :].bitcast(I32),
                 )
+
+        def load_bias(part):
+            cols = slice(part * HEADS_PER_W_LOAD * P, (part + 1) * HEADS_PER_W_LOAD * P)
+            nc.sync.dma_start(out=bias[:, cols], in_=bv[cols].partition_broadcast(P))
 
         def load_w(part):
             cols = slice(part * HEADS_PER_W_LOAD * P, (part + 1) * HEADS_PER_W_LOAD * P)
@@ -405,9 +409,10 @@ def tile_flashattentionmodule_pa_kernel(
         for g in range(X_PASSES):
             load_x(g)
         load_cached_values(0)
+        load_keys_and_queries(2)
         load_w_scales()
         load_w(0)
-        nc.sync.dma_start(out=bias[:], in_=bv.partition_broadcast(P))
+        load_bias(0)
         load_cached_values(1)
 
         columns[0] = work.tile([P, 2 * PAST], BF16, tag="columns", name="columns")
@@ -437,10 +442,12 @@ def tile_flashattentionmodule_pa_kernel(
             turns_operands = 1 <= next_head < HEADS and piece % 2 == 0
             refills = [divmod(UNIT_BANKS * now + SCORE_BANKS + n, UNIT_BANKS) for n in range(UNIT_BANKS)]
 
-            if block == 0 and is_head(h) and is_head(h + 2):
-                if (h + 2) % HEADS_PER_W_LOAD == 0:
+            if block == 0 and is_head(h):
+                if is_head(h + 3):
+                    load_keys_and_queries(h + 3)
+                if is_head(h + 2) and (h + 2) % HEADS_PER_W_LOAD == 0:
                     load_w((h + 2) // HEADS_PER_W_LOAD)
-                load_keys_and_queries(h + 2)
+                    load_bias((h + 2) // HEADS_PER_W_LOAD)
             if block == 0 and is_head(h):
                 for late in range(2 if h == 0 else h + VALUE_LEAD + 1, h + VALUE_LEAD + 2):
                     if is_head(late):
@@ -516,15 +523,15 @@ def tile_flashattentionmodule_pa_kernel(
                 join_maxima(ahead)
             if 1 <= now <= X_PASSES:
                 quantise_x(now - 1)
-            if 2 <= now <= VALUE_LEAD + 2:
-                quantise_cached_values(now - 2)
+            if 3 <= now <= VALUE_LEAD + 3:
+                quantise_cached_values(now - 3)
             if head_at(now, 3) >= 0:
                 quantise_e(head_at(now, 3), 0)
             if head_at(now, 5) >= 0:
                 quantise_e(head_at(now, 5), 1)
-            if 1 <= now <= VALUE_LEAD + 1:
-                group_cached_values(now - 1, 0)
-                group_cached_values(now - 1, 1)
+            if 2 <= now <= VALUE_LEAD + 2:
+                group_cached_values(now - 2, 0)
+                group_cached_values(now - 2, 1)
             if head_at(now, 8) >= 0:
                 normalise(head_at(now, 8))
                 store(head_at(now, 8))

from contextlib import ExitStack
import math

import concourse.mybir as mybir
from concourse.masks import make_identity

F32 = mybir.dt.float32
BF16 = mybir.dt.bfloat16
I32 = mybir.dt.int32
U32 = mybir.dt.uint32
U8 = mybir.dt.uint8
FP8X4 = mybir.dt.float8_e4m3fn_x4
ALU = mybir.AluOpType
ACT = mybir.ActivationFunctionType
AX = mybir.AxisListType

P = 128
HEADS = 16
NEW = 512
PAST = 1024
FEATURES = 2048
BANK = 512
K_PASS = 512
Q_BLOCKS = NEW // P
KEY_PASSES = (PAST + NEW) // K_PASS
X_PASSES = FEATURES // K_PASS
HEADS_PER_W_LOAD = 2
UNITS = HEADS * Q_BLOCKS
UNIT_BANKS = 3
SCORE_BANKS = 5
QUARTER_ORDER = (3, 0, 1, 2)
QUARTER_PAIRS = ((0, 3), (1, 2))
SCALE = 1.0 / math.sqrt(P)
VALUE_LEAD = 1
LAST = HEADS - 1
E_PARTS = ((0, 2048), (2048, 2048), (4096, 1024), (5120, 1024))
LAST_E_PARTS = ((0, 2048), (2048, 2048), (4096, 512), (4608, 1024), (5632, 512))
LOWEST = -3.0e38
MASKED = -1.0e10

FLOPS = 2 * NEW * FEATURES * FEATURES + 2 * 2 * HEADS * NEW * (PAST + NEW) * P


def tile_flashattentionmodule_pa_kernel(
    tc, x, q, k_new, past_k, past_v, Wv_words, Wv_scales, bv, out
):
    nc = tc.nc
    with ExitStack() as ctx:
        ctx.enter_context(tc.manual_schedule())
        const = ctx.enter_context(tc.tile_pool(name="const", bufs=1))
        raw = ctx.enter_context(tc.tile_pool(name="raw", bufs=4))
        work = ctx.enter_context(tc.tile_pool(name="work", bufs=2))
        small = ctx.enter_context(tc.tile_pool(name="small", bufs=4))
        score_pool = ctx.enter_context(tc.psum_pool(name="score_pool", bufs=SCORE_BANKS - 1))
        new_score_pool = ctx.enter_context(tc.psum_pool(name="new_score_pool", bufs=1))
        other_pool = ctx.enter_context(tc.psum_pool(name="other_pool", bufs=1))

        ident_bf = const.tile([P, P], BF16, name="ident_bf")
        make_identity(nc, ident_bf[:])
        ident_f32 = const.tile([P, P], F32, name="ident_f32")
        make_identity(nc, ident_f32[:])
        causal_f32 = const.tile([P, P], F32, name="causal_f32")
        nc.gpsimd.memset(causal_f32[:], 0.0)
        nc.gpsimd.affine_select(
            out=causal_f32[:],
            in_=causal_f32[:],
            compare_op=ALU.is_ge,
            fill=MASKED,
            base=0,
            pattern=[[-1, P]],
            channel_multiplier=1,
        )
        causal = const.tile([P, P], BF16, name="causal")
        nc.vector.tensor_copy(out=causal[:], in_=causal_f32[:])

        join_factors = const.tile([P, UNIT_BANKS], F32, name="join_factors")
        nc.vector.memset(join_factors[:, 0 : UNIT_BANKS - 1], 1.0)
        nc.vector.memset(join_factors[:, UNIT_BANKS - 1 :], -SCALE)

        w_scales = const.tile([P, FEATURES], U8, name="w_scales", align_bytes=64)
        nc.vector.memset(w_scales[:].bitcast(I32), 0)

        e_tiles = []
        for i in range(Q_BLOCKS):
            e_tile = const.tile([P, PAST + NEW], BF16, name="e_block%d" % i)
            if i + 1 < Q_BLOCKS:
                nc.vector.memset(e_tile[:, PAST + P * (i + 1) :], 0.0)
            e_tiles.append(e_tile)

        x_rows = []
        for g in range(X_PASSES):
            x_slice = const.tile([P, 4, K_PASS], BF16, name="x_rows%d" % g)
            x_rows.append(x_slice)
        x_words = const.tile([P, X_PASSES, NEW], U32, name="x_words", align_bytes=64)
        x_scales = const.tile([P, X_PASSES, NEW], U8, name="x_scales", align_bytes=64)
        w_words = const.tile([P, X_PASSES, FEATURES], U32, name="w_words", align_bytes=64)
        bias = const.tile([P, FEATURES], BF16, name="bias")

        k_past, k_fresh, q_rows, v_past = {}, {}, {}, {}
        columns = {}
        v_grouped, v_words, v_scales = {}, {}, {}
        e_words, e_scales, sums, inverse, result = {}, {}, {}, {}, {}
        x_banks, x_grouped = {}, {}
        y, o = {}, {}
        score_banks = {}
        bank_max, shift = {}, {}
        row_sum = {}
        e_grouped = {}

        def load_keys_and_queries(h):
            q_rows[h] = raw.tile([P, Q_BLOCKS, P], BF16, tag="q_rows", name="q_rows")
            nc.sync.dma_start(out=q_rows[h][:], in_=q[0, h].rearrange("(i r) d -> r i d", r=P))
            k_past[h] = raw.tile([P, 2, 4, P], BF16, tag="k_past", name="k_past")
            nc.sync.dma_start(
                out=k_past[h][:], in_=past_k[0, h].rearrange("(a r c) d -> r a c d", a=2, c=4)
            )
            k_fresh[h] = raw.tile([P, Q_BLOCKS, P], BF16, tag="k_fresh", name="k_fresh")
            nc.sync.dma_start(out=k_fresh[h][:], in_=k_new[0, h].rearrange("(j r) d -> r j d", r=P))

        def load_cached_values(h):
            v_past[h] = raw.tile([P, 8, P], BF16, tag="v_past", name="v_past", bufs=VALUE_LEAD + 2)
            nc.sync.dma_start(out=v_past[h][:], in_=past_v[0, h].rearrange("(p j) d -> p j d", j=8))

        def load_x(g):
            by_part = x[0].rearrange("(u m c) k -> u m c k", u=2, c=2)
            for u in range(2):
                nc.sync.dma_start(
                    out=x_rows[g][:, 2 * u : 2 * u + 2, :], in_=by_part[u][:, :, K_PASS * g : K_PASS * (g + 1)]
                )

        def load_w_scales():
            for quadrant in range(4):
                nc.sync.dma_start(
                    out=w_scales[32 * quadrant : 32 * quadrant + 16, :].bitcast(I32),
                    in_=Wv_scales[:, 4 * quadrant : 4 * quadrant + 4, :].bitcast(I32),
                )

        def load_bias(part):
            cols = slice(part * HEADS_PER_W_LOAD * P, (part + 1) * HEADS_PER_W_LOAD * P)
            nc.sync.dma_start(out=bias[:, cols], in_=bv[cols].partition_broadcast(P))

        def load_w(part):
            cols = slice(part * HEADS_PER_W_LOAD * P, (part + 1) * HEADS_PER_W_LOAD * P)
            nc.sync.dma_start(
                out=w_words[:, :, cols].bitcast(I32),
                in_=Wv_words.rearrange("g p n t -> p g (n t)").bitcast(I32)[:, :, cols],
            )

        def turn_x(g, half):
            if half == 0:
                x_grouped[g] = work.tile([P, NEW, 4], BF16, tag="x_grouped", name="x_grouped", align_bytes=64)
            bank = other_pool.tile([P, 2, 2, P], F32, tag="mx_bank", name="x_bank")
            for part in range(2):
                pairs = x_rows[g][:, 2 * half + part, :].bitcast(F32)
                for u in range(2):
                    nc.tensor.transpose(bank[:, part, u, :], pairs[:, u : K_PASS // 2 : 2], ident_f32[:])
            x_banks[(g, half)] = bank

        def group_x(g, half, copy):
            copy(
                out=x_grouped[g][:, 256 * half : 256 * (half + 1), :]
                .bitcast(F32)
                .rearrange("p (part m) u -> p part m u", part=2),
                in_=x_banks[(g, half)][:].rearrange("p part u m -> p part m u"),
            )

        def quantise_x(g):
            nc.vector.quantize_mx(
                out=x_words[:, g, :].bitcast(FP8X4),
                scales=x_scales[:, g, :],
                in_=x_grouped[g][:].rearrange("p m t -> p (m t)"),
            )

        def operand_rows(h, position):
            if position < 8:
                c, a = divmod(position, 2)
                return k_past[h][:, a, c, :]
            if position < 12:
                return k_fresh[h][:, position - 8, :]
            return q_rows[h][:, position - 12, :]

        def turn_operands(h, quarter, half_bank):
            for j in range(4):
                nc.tensor.transpose(half_bank[:, j, :], operand_rows(h, 4 * quarter + j), ident_bf[:])

        def copy_operands(h, quarter, half_bank, on_vector=False):
            copy = nc.vector.tensor_copy if on_vector else nc.scalar.copy
            copy(
                out=columns[h][:, BANK * quarter : BANK * (quarter + 1)],
                in_=half_bank.rearrange("p j r -> p (j r)"),
            )

        def copy_operand_pair(h, pair, bank):
            nc.scalar.copy(
                out=columns[h][:].rearrange("p (a c) -> p a c", a=4)[:, pair[0] : pair[1] + 1 : pair[1] - pair[0]],
                in_=bank[:].rearrange("p n j r -> p n (j r)"),
            )

        def group_cached_values(h, g):
            if g == 0:
                v_grouped[h] = work.tile(
                    [P, KEY_PASSES, P, 4], BF16, tag="v_grouped", name="v_grouped", bufs=VALUE_LEAD + 3, align_bytes=64
                )
            nc.vector.tensor_copy(
                out=v_grouped[h][:, g].rearrange("p (n i) (u c) -> p n u c i", i=4, u=2),
                in_=v_past[h][:].rearrange("p (c g u) (n i) -> p g n u c i", c=2, g=2, i=4)[:, g],
            )

        def quantise_cached_values(h):
            v_words[h] = work.tile(
                [P, KEY_PASSES, P], U32, tag="v_words", name="v_words", bufs=VALUE_LEAD + 3, align_bytes=64
            )
            v_scales[h] = work.tile(
                [P, KEY_PASSES, P], U8, tag="v_scales", name="v_scales", bufs=VALUE_LEAD + 3, align_bytes=64
            )
            nc.vector.quantize_mx(
                out=v_words[h][:, 0:2, :].rearrange("p g d -> p (g d)").bitcast(FP8X4),
                scales=v_scales[h][:, 0:2, :].rearrange("p g d -> p (g d)"),
                in_=v_grouped[h][:, 0:2].rearrange("p g d t -> p (g d t)"),
            )

        def project_new_values(h, u):
            if u == 0 and h == HEADS - 1:
                y[h] = score_pool.tile([P, 4, P], F32, tag="s", name="y_last")
            elif u == 0:
                y[h] = other_pool.tile([P, 4, P], F32, tag="mx_bank", name="y")
            cols = slice(P * h, P * (h + 1))
            for c in range(2):
                tokens = slice(P * (2 * u + c), P * (2 * u + c + 1))
                for g in range(X_PASSES):
                    nc.tensor.matmul_mx(
                        out=y[h][:, 2 * u + c, :],
                        lhsT=x_words[:, g, tokens].bitcast(FP8X4),
                        lhsT_scale=x_scales[:, g, tokens],
                        rhs=w_words[:, g, cols].bitcast(FP8X4),
                        rhs_scale=w_scales[4 * g : P, cols],
                        start=(g == 0),
                        stop=(g == X_PASSES - 1),
                    )

        def group_new_values(h):
            nc.vector.tensor_tensor(
                out=v_grouped[h][:, 2],
                in0=y[h][:].rearrange("p t d -> p d t"),
                in1=bias[:, P * h : P * (h + 1)].unsqueeze(2).to_broadcast([P, P, 4]),
                op=ALU.add,
            )

        def quantise_new_values(h):
            nc.vector.quantize_mx(
                out=v_words[h][:, 2, :].bitcast(FP8X4),
                scales=v_scales[h][:, 2, :],
                in_=v_grouped[h][:, 2].rearrange("p d t -> p (d t)"),
            )

        def score_bank(unit, c):
            h, i = divmod(unit, Q_BLOCKS)
            queries = columns[h][:, PAST + NEW + P * i : PAST + NEW + P * (i + 1)]
            if c < PAST // BANK:
                s = score_pool.tile([P, BANK], F32, tag="s", name="s")
            else:
                s = new_score_pool.tile([P, BANK], F32, tag="s_new", name="s_new")
            if c < PAST // BANK:
                width = BANK
                nc.tensor.matmul(
                    out=s[:], lhsT=queries, rhs=columns[h][:, BANK * c : BANK * (c + 1)], start=True, stop=True
                )
            else:
                width = P * (i + 1)
                nc.tensor.matmul(
                    out=s[:, 0:width], lhsT=queries, rhs=columns[h][:, PAST : PAST + width], start=True, stop=False
                )
                nc.tensor.matmul(
                    out=s[:, width - P : width], lhsT=ident_bf[:], rhs=causal[:], start=False, stop=True
                )
            score_banks[(unit, c)] = (s, width)

        def bank_maximum(unit, c):
            if unit not in bank_max:
                bank_max[unit] = small.tile([P, UNIT_BANKS], F32, tag="bank_max", name="bank_max")
            s, width = score_banks[(unit, c)]
            nc.vector.reduce_max(out=bank_max[unit][:, c : c + 1], in_=s[:, 0:width], axis=AX.X)

        def join_maxima(unit):
            joined = small.tile([P, UNIT_BANKS], F32, tag="joined", name="joined")
            nc.vector.tensor_tensor_scan(
                out=joined[:],
                data0=bank_max[unit][:],
                data1=join_factors[:],
                initial=LOWEST,
                op0=ALU.max,
                op1=ALU.mult,
            )
            shift[unit] = joined[:, UNIT_BANKS - 1 : UNIT_BANKS]

        def exponentials(unit):
            h, i = divmod(unit, Q_BLOCKS)
            if i == 0:
                sums[h] = small.tile([P, Q_BLOCKS, UNIT_BANKS], F32, tag="sums", name="sums")
            for c in (2, 0, 1):
                s, width = score_banks[(unit, c)]
                nc.scalar.activation(
                    out=e_tiles[i][:, BANK * c : BANK * c + width],
                    in_=s[:, 0:width],
                    func=ACT.Exp,
                    bias=shift[unit],
                    scale=SCALE,
                    accum_out=sums[h][:, i, c : c + 1],
                )

        def turn_e(unit, first, count, bank):
            pairs = e_tiles[unit % Q_BLOCKS][:].bitcast(F32)
            for g in range(count):
                for u in range(2):
                    left = P * (2 * (first + g) + u)
                    nc.tensor.transpose(bank[:, g, u, :], pairs[:, left : left + P], ident_f32[:])

        def group_e(unit, first, count, bank):
            h, i = divmod(unit, Q_BLOCKS)
            nc.scalar.copy(
                out=e_grouped[h][:, i, first : first + count].bitcast(F32),
                in_=bank.rearrange("p g u q -> p g q u"),
            )

        def group_third_passes(unit, bank):
            h, i = divmod(unit, Q_BLOCKS)
            nc.scalar.copy(
                out=e_grouped[h][:, i - 1 : i + 1, 2].bitcast(F32),
                in_=bank[:].rearrange("p n u q -> p n q u"),
            )

        def quantise_e(h, part):
            left, width = (LAST_E_PARTS if h == LAST else E_PARTS)[part]
            words = slice(left // 4, (left + width) // 4)
            if h not in e_words:
                e_words[h] = work.tile(
                    [P, Q_BLOCKS, KEY_PASSES, P], U32, tag="e_words", name="e_words", bufs=3, align_bytes=64
                )
                e_scales[h] = work.tile(
                    [P, Q_BLOCKS, KEY_PASSES, P], U8, tag="e_scales", name="e_scales", bufs=3, align_bytes=64
                )
            nc.vector.quantize_mx(
                out=e_words[h][:].rearrange("p i g q -> p (i g q)")[:, words].bitcast(FP8X4),
                scales=e_scales[h][:].rearrange("p i g q -> p (i g q)")[:, words],
                in_=e_grouped[h][:].rearrange("p i g q t -> p (i g q t)")[:, left : left + width],
            )

        def weighted_block(h, i, sums_out):
            for g in range(KEY_PASSES):
                nc.tensor.matmul_mx(
                    out=sums_out,
                    lhsT=e_words[h][:, i, g, :].bitcast(FP8X4),
                    lhsT_scale=e_scales[h][:, i, g, :],
                    rhs=v_words[h][:, g, :].bitcast(FP8X4),
                    rhs_scale=v_scales[h][:, g, :],
                    start=(g == 0),
                    stop=(g == KEY_PASSES - 1),
                )

        def weighted_values(h, half):
            if half == 0:
                o[h] = other_pool.tile([P, Q_BLOCKS, P], F32, tag="mx_bank", name="o")
            for i in (2 * half, 2 * half + 1):
                weighted_block(h, i, o[h][:, i, :])

        def add_sums(h):
            row_sum[h] = small.tile([P, Q_BLOCKS], F32, tag="row_sum", name="row_sum")
            nc.vector.reduce_sum(out=row_sum[h][:], in_=sums[h][:], axis=AX.X)

        def invert_sums(h):
            inverse[h] = small.tile([P, Q_BLOCKS], F32, tag="inverse", name="inverse")
            nc.vector.reciprocal(out=inverse[h][:], in_=row_sum[h][:])

        def divide(h, first, count, sums_in, quotient):
            nc.vector.tensor_tensor(
                out=quotient[:],
                in0=sums_in[:],
                in1=inverse[h][:, first : first + count].unsqueeze(2).to_broadcast([P, count, P]),
                op=ALU.mult,
            )

        def normalise(h):
            result[h] = work.tile([P, Q_BLOCKS, P], F32, tag="result", name="result")
            divide(h, 0, Q_BLOCKS, o[h], result[h])

        def normalise_on_scalar(h, first, count, sums_in, quotient):
            for n in range(count):
                nc.scalar.activation(
                    out=quotient[:, n, :],
                    in_=sums_in[:, n, :],
                    func=ACT.Copy,
                    scale=inverse[h][:, first + n : first + n + 1],
                )

        def store(h, first=0, count=Q_BLOCKS, quotient=None):
            nc.sync.dma_start(
                out=out[0].rearrange("(i r) (h d) -> h r i d", r=P, d=P)[h][:, first : first + count, :],
                in_=(result[h] if quotient is None else quotient)[:],
            )

        def is_unit(unit):
            return 0 <= unit < UNITS

        def is_head(h):
            return 0 <= h < HEADS

        load_keys_and_queries(0)
        load_keys_and_queries(1)
        for g in range(X_PASSES):
            load_x(g)
        load_cached_values(0)
        load_keys_and_queries(2)
        load_w_scales()
        load_w(0)
        load_bias(0)
        load_cached_values(1)

        columns[0] = work.tile([P, 2 * PAST], BF16, tag="columns", name="columns")
        for n, quarter in enumerate(QUARTER_ORDER):
            if n < 3:
                operand_bank = other_pool.tile(
                    [P, 4, P], BF16, tag=("e_bank", "shared_bank", "mx_bank")[n], name="operand_bank"
                )
            else:
                operand_bank = score_pool.tile([P, 4, P], BF16, tag="s", name="operand_bank")
            turn_operands(0, quarter, operand_bank[:])
            copy_operands(0, quarter, operand_bank[:], on_vector=(n % 2 == 1))

        def head_at(now, offset):
            j, rest = divmod(now - offset, Q_BLOCKS)
            return j if rest == 0 and is_head(j) else -1

        def ahead_of(now, offset):
            j = head_at(now, offset)
            return j + VALUE_LEAD if j >= 1 and is_head(j + VALUE_LEAD) else -1

        for now in range(-2, UNITS - 1):
            h, block = divmod(now, Q_BLOCKS)
            behind = now - 1
            ahead = now + 1
            next_head, piece = divmod(now + 1 + Q_BLOCKS, Q_BLOCKS)
            turns_operands = 1 <= next_head < HEADS and piece % 2 == 0
            refills = [divmod(UNIT_BANKS * now + SCORE_BANKS + n, UNIT_BANKS) for n in range(UNIT_BANKS)]

            if block == 0 and is_head(h):
                if is_head(h + 3):
                    load_keys_and_queries(h + 3)
                if is_head(h + 2) and (h + 2) % HEADS_PER_W_LOAD == 0:
                    load_w((h + 2) // HEADS_PER_W_LOAD)
                    load_bias((h + 2) // HEADS_PER_W_LOAD)
            if block == 0 and is_head(h):
                for late in range(2 if h == 0 else h + VALUE_LEAD + 1, h + VALUE_LEAD + 2):
                    if is_head(late):
                        load_cached_values(late)

            if is_unit(behind):
                if behind % Q_BLOCKS == 0:
                    e_grouped[behind // Q_BLOCKS] = work.tile(
                        [P, Q_BLOCKS, KEY_PASSES, P, 4], BF16, tag="e_grouped", name="e_grouped", align_bytes=64
                    )
                e_bank = other_pool.tile([P, 2, 2, P], F32, tag="e_bank", name="e_bank")
                turn_e(behind, 0, 2, e_bank[:])
            if is_unit(behind) and behind % 2 == 1:
                third_bank = other_pool.tile([P, 2, 2, P], F32, tag="shared_bank", name="third_bank")
                turn_e(behind - 1, 2, 1, third_bank[:, 0:1])
                turn_e(behind, 2, 1, third_bank[:, 1:2])
            if turns_operands:
                if piece == 0:
                    columns[next_head] = work.tile([P, 2 * PAST], BF16, tag="columns", name="columns")
                pair = QUARTER_PAIRS[piece // 2]
                pair_bank = other_pool.tile([P, 2, 4, P], BF16, tag="shared_bank", name="pair_bank")
                for n in range(2):
                    turn_operands(next_head, pair[n], pair_bank[:, n])

            if is_unit(now):
                exponentials(now)
            if is_unit(behind):
                group_e(behind, 0, 2, e_bank[:])
            if turns_operands:
                copy_operand_pair(next_head, pair, pair_bank)
            if is_unit(behind) and behind % 2 == 1:
                group_third_passes(behind, third_bank)
            if is_unit(refills[0][0]):
                score_bank(*refills[0])
            if 0 <= now < X_PASSES:
                turn_x(now, 0)
            if 0 <= head_at(now, 5) < LAST:
                project_new_values(head_at(now, 5), 0)
            if 0 <= head_at(now, 6) < LAST:
                project_new_values(head_at(now, 6), 1)
            if 0 <= head_at(now, 7) < LAST - 1:
                weighted_values(head_at(now, 7), 0)
            if 0 <= head_at(now, 8) < LAST - 1:
                weighted_values(head_at(now, 8), 1)
            if now == UNITS - 2:
                project_new_values(LAST, 0)
                project_new_values(LAST, 1)
            if 0 <= now < X_PASSES:
                turn_x(now, 1)
                group_x(now, 1, nc.scalar.copy)
            if is_unit(refills[1][0]):
                score_bank(*refills[1])
            if is_unit(refills[2][0]):
                score_bank(*refills[2])
            if is_unit(ahead):
                bank_maximum(ahead, 0 if ahead == 0 else 1)
                bank_maximum(ahead, 1 if ahead == 0 else 0)
            if is_unit(ahead):
                bank_maximum(ahead, 2)
            if ahead_of(now, 4) >= 0:
                quantise_cached_values(ahead_of(now, 4))
            if ahead_of(now, 1) >= 0:
                group_cached_values(ahead_of(now, 1), 0)
            if head_at(now, 6) >= 0:
                quantise_e(head_at(now, 6), 2)
            if ahead_of(now, 3) >= 0:
                group_cached_values(ahead_of(now, 3), 1)
            if head_at(now, 7) >= 0:
                invert_sums(head_at(now, 7))
            if 0 <= now < X_PASSES:
                group_x(now, 0, nc.vector.tensor_copy)
            if is_unit(ahead):
                join_maxima(ahead)
            if 1 <= now <= X_PASSES:
                quantise_x(now - 1)
            if 3 <= now <= VALUE_LEAD + 3:
                quantise_cached_values(now - 3)
            if head_at(now, 3) >= 0:
                quantise_e(head_at(now, 3), 0)
            if head_at(now, 5) >= 0:
                quantise_e(head_at(now, 5), 1)
            if 2 <= now <= VALUE_LEAD + 2:
                group_cached_values(now - 2, 0)
                group_cached_values(now - 2, 1)
            if head_at(now, 8) >= 0:
                normalise(head_at(now, 8))
                store(head_at(now, 8))
            if head_at(now, 5) >= 0:
                add_sums(head_at(now, 5))
            if head_at(now, 6) >= 0:
                group_new_values(head_at(now, 6))
                quantise_e(head_at(now, 6), 3)
                quantise_new_values(head_at(now, 6))

        before = UNITS - 2
        last = UNITS - 1
        e_bank = other_pool.tile([P, 2, 2, P], F32, tag="e_bank", name="e_bank")
        turn_e(before, 0, 2, e_bank[:])
        third_before = other_pool.tile([P, 1, 2, P], F32, tag="shared_bank", name="third_before")
        turn_e(before, 2, 1, third_before[:])

        exponentials(last)

        invert_sums(LAST - 1)
        quantise_e(LAST, 0)
        group_new_values(LAST)

        e_last = score_pool.tile([P, 2, 2, P], F32, tag="s", name="e_last")
        turn_e(last, 0, 2, e_last[:])
        third_last = score_pool.tile([P, 1, 2, P], F32, tag="s", name="third_last")
        turn_e(last, 2, 1, third_last[:])
        weighted_values(LAST - 1, 0)
        weighted_values(LAST - 1, 1)
        group_e(before, 0, 2, e_bank[:])
        group_e(before, 2, 1, third_before[:])
        group_e(last, 0, 2, e_last[:])
        group_e(last, 2, 1, third_last[:])
        result[LAST - 1] = work.tile([P, Q_BLOCKS, P], F32, tag="result", name="result")
        normalise_on_scalar(LAST - 1, 0, Q_BLOCKS, o[LAST - 1], result[LAST - 1])
        store(LAST - 1)

        quantise_new_values(LAST)
        quantise_e(LAST, 1)
        add_sums(LAST)
        quantise_e(LAST, 2)
        quantise_e(LAST, 3)
        invert_sums(LAST)
        quantise_e(LAST, 4)

        for first, count in ((0, 2), (2, 1), (3, 1)):
            sums_in = score_pool.tile([P, count, P], F32, tag="s", name="o_part")
            for n in range(count):
                weighted_block(LAST, first + n, sums_in[:, n, :])
            quotient = work.tile([P, count, P], F32, tag="result_%d" % first, name="quotient")
            divide(LAST, first, count, sums_in, quotient)
            store(LAST, first, count, quotient)
